import numpy as np
import ml_dtypes


def mxq(x, axis, fmt="e4m3"):
    dtype, down = {"e4m3": (ml_dtypes.float8_e4m3fn, 7), "e5m2": (ml_dtypes.float8_e5m2, 14)}[fmt]
    v = np.moveaxis(np.asarray(x, np.float32).astype(ml_dtypes.bfloat16).astype(np.float64), axis, -1)
    blocks = v.reshape(v.shape[:-1] + (-1, 32))
    amax = np.abs(blocks).max(-1, keepdims=True)
    byte = np.maximum(np.where(amax > 0, np.frexp(amax)[1] - 1 + 127, 0) - down, 1)
    scale = np.exp2(byte - 127.0)
    codes = (blocks / scale).astype(np.float32).astype(dtype).astype(np.float64)
    return np.moveaxis((codes * scale).reshape(v.shape), -1, axis)


WIDE = False


def mx_kscale(k):
    if not WIDE:
        return np.ones(k)
    levels = np.array([10, -10, 5, -5, 0])
    a = np.random.permutation(np.resize(levels, k // 512 * 4)).reshape(k // 512, 4)
    idx = np.arange(k)
    return np.exp2(a[idx // 512, idx % 128 // 32])


BF16 = ml_dtypes.bfloat16


def bf(x):
    return np.asarray(x, np.float32).astype(BF16)


def f64(x):
    return np.asarray(x).astype(np.float64)


B, IN_DIM, R_IN, R_OUT = 4096, 1024, 512, 512
HIDDEN = R_IN + R_OUT
BASELINE_THRE = 0.1
BETA = 1.8
R_M = 3.0
DT = 1.0


def sigmoid(v):
    return 1.0 / (1.0 + np.exp(-v))


def setup_inputs():
    s = mx_kscale(IN_DIM)
    return {
        "x_t": bf(np.random.standard_normal((B, IN_DIM)) * s),
        "spk_t": bf(np.random.random((B, HIDDEN)) < 0.3),
        "mem_t_in": bf(np.random.standard_normal((B, R_IN))),
        "b_t_in": bf(np.random.random((B, R_IN))),
        "W_x2in": bf(np.random.standard_normal((R_IN, IN_DIM)) / np.sqrt(IN_DIM) / s[None, :]),
        "b_x2in": bf(np.random.standard_normal(R_IN) * 0.5),
        "W_rec4in": bf(np.random.standard_normal((R_IN, R_IN)) * 1.5 / np.sqrt(R_IN)),
        "b_rec4in": bf(np.random.standard_normal(R_IN) * 0.5),
        "W_out2in": bf(np.random.standard_normal((R_IN, R_OUT)) * 1.5 / np.sqrt(R_OUT)),
        "b_out2in": bf(np.random.standard_normal(R_IN) * 0.5),
        "tau_adp_in": bf(1.5 + 0.5 * np.random.standard_normal(R_IN)),
        "tau_m_in": bf(2.0 + 0.5 * np.random.standard_normal(R_IN)),
    }


def reference(x_t, spk_t, mem_t_in, b_t_in, W_x2in, b_x2in, W_rec4in, b_rec4in, W_out2in, b_out2in, tau_adp_in, tau_m_in):
    spk = f64(spk_t)
    spk_out = spk[:, :R_OUT]
    spk_in = spk[:, R_OUT:]
    x = (mxq(f64(x_t), 1, "e4m3") @ mxq(f64(W_x2in), 1, "e4m3").T) + f64(b_x2in)
    rec = (mxq(spk_in, 1, "e4m3") @ mxq(f64(W_rec4in), 1, "e4m3").T) + f64(b_rec4in)
    fbk = (mxq(spk_out, 1, "e4m3") @ mxq(f64(W_out2in), 1, "e4m3").T) + f64(b_out2in)
    r_in_ = x + rec + fbk
    tau_m_s = sigmoid(f64(tau_m_in))
    tau_adp_s = sigmoid(f64(tau_adp_in))
    b = tau_adp_s * f64(b_t_in) + (1.0 - tau_adp_s) * spk_in
    new_thre = BASELINE_THRE + BETA * b
    mem = f64(mem_t_in) * tau_m_s + (1.0 - tau_m_s) * R_M * r_in_ - new_thre * spk_in * DT
    return mem

@@ -1,0 +1,252 @@
+from contextlib import ExitStack
+
+import concourse.mybir as mybir
+from concourse.masks import make_identity
+
+F32 = mybir.dt.float32
+BF16 = mybir.dt.bfloat16
+U32 = mybir.dt.uint32
+U8 = mybir.dt.uint8
+FP8X4 = mybir.dt.float8_e4m3fn_x4
+ALU = mybir.AluOpType
+ACT = mybir.ActivationFunctionType
+
+P = 128
+B, IN_DIM, R_IN = 4096, 1024, 512
+GS = 512
+G = B // GS
+FLOPS = 2 * B * (IN_DIM + 2 * R_IN) * R_IN
+
+PASS_ORDER = (3, 2, 0, 1)
+TX_ON_VECTOR = (2, 6)
+Y3_ON_GPSIMD = ()
+E_ON_GPSIMD = (0, 1, 2, 3)
+FINAL_ON_VECTOR = ()
+
+
+def tile_snnlayer_pa_t_kernel(
+    tc, x_t, spk_t, mem_t_in, b_t_in, W_x2in, b_x2in, W_rec4in, b_rec4in, W_out2in, b_out2in, tau_adp_in, tau_m_in, out
+):
+    nc = tc.nc
+    with ExitStack() as ctx:
+        const = ctx.enter_context(tc.tile_pool(name="const", bufs=1))
+        wpool = ctx.enter_context(tc.tile_pool(name="wpool", bufs=1))
+        ld = ctx.enter_context(tc.tile_pool(name="ld", bufs=3))
+        qp = ctx.enter_context(tc.tile_pool(name="qp", bufs=2))
+        ep = ctx.enter_context(tc.tile_pool(name="ep", bufs=2))
+        ps = ctx.enter_context(tc.psum_pool(name="ps", bufs=1))
+
+        def tx_bank(name):
+            return ps.tile([P, 512], F32, name=name, tag="tx", bufs=3)
+
+        loaded = {}
+
+        def load(g):
+            rows = slice(g * GS, (g + 1) * GS)
+            ss = ld.tile([P, 4 * 1024], BF16, name="ss", tag="ss")
+            xs = ld.tile([P, 4 * 1024], BF16, name="xs", tag="xs")
+            bs = ld.tile([P, 4 * 512], BF16, name="bs", tag="bs")
+            ms = ld.tile([P, 4 * 512], BF16, name="ms", tag="ms")
+            for dst, src in ((ss, spk_t), (xs, x_t), (bs, b_t_in), (ms, mem_t_in)):
+                nc.sync.dma_start(
+                    out=dst[:].rearrange("p (t k) -> p t k", t=4),
+                    in_=src[rows, :].rearrange("(p t) k -> p t k", t=4),
+                )
+            loaded[g] = (xs, ss, bs, ms)
+
+        ident = const.tile([P, P], F32, name="ident")
+        make_identity(nc, ident[:])
+
+        craw = const.tile([P, 256], BF16, name="craw")
+        nc.vector.memset(craw[:], 0.0)
+        for v, vec in enumerate((b_x2in, b_rec4in, b_out2in, tau_adp_in, tau_m_in)):
+            nc.scalar.dma_start(out=craw[2 * v : 2 * v + 2, :], in_=vec.rearrange("(u w) -> u w", u=2))
+
+        load(0)
+        wx = wpool.tile([P, 4 * 1024], BF16, name="wx")
+        wo = wpool.tile([P, 4 * 512], BF16, name="wo")
+        wr = wpool.tile([P, 4 * 512], BF16, name="wr")
+        for dst, src in ((wr, W_rec4in), (wo, W_out2in), (wx, W_x2in)):
+            nc.sync.dma_start(
+                out=dst[:].rearrange("p (u e k) -> p u e k", u=2, e=2),
+                in_=src.rearrange("(u p e) k -> p u e k", u=2, p=P, e=2),
+            )
+        load(1)
+
+        cps = tx_bank("cps")
+        nc.tensor.transpose(cps[:, 0:P], craw[:].bitcast(F32), ident[:])
+        cst = const.tile([P, 20], F32, name="cst")
+        nc.vector.tensor_copy(out=cst[:], in_=cps[:].bitcast(BF16)[:, 0:20])
+        bsum = const.tile([P, 4], F32, name="bsum")
+        nc.vector.tensor_add(out=bsum[:], in0=cst[:, 0:4], in1=cst[:, 4:8])
+        nc.vector.tensor_add(out=bsum[:], in0=bsum[:], in1=cst[:, 8:12])
+        sg = const.tile([P, 8], F32, name="sg")
+        ng = const.tile([P, 8], F32, name="ng")
+        nc.scalar.activation(out=sg[:], in_=cst[:, 12:20], func=ACT.Sigmoid)
+        nc.scalar.activation(out=ng[:], in_=cst[:, 12:20], func=ACT.Sigmoid, scale=-1.0)
+        pq = const.tile([P, 4], F32, name="pq")
+        qq = const.tile([P, 4], F32, name="qq")
+        c3 = const.tile([P, 4], F32, name="c3")
+        k0 = const.tile([P, 4], F32, name="k0")
+        nc.vector.tensor_scalar_mul(out=pq[:], in0=sg[:, 0:4], scalar1=1.8)
+        nc.vector.tensor_scalar_mul(out=qq[:], in0=ng[:, 0:4], scalar1=1.8)
+        nc.vector.tensor_scalar_mul(out=c3[:], in0=ng[:, 4:8], scalar1=3.0)
+        nc.vector.tensor_mul(out=k0[:], in0=c3[:], in1=bsum[:])
+        aa = sg[:, 4:8]
+
+        gw = wpool.tile([P, 16 * 512], BF16, name="gw", align_bytes=64)
+        wcodes = wpool.tile([P, 16 * P], U32, name="wcodes", align_bytes=64)
+        wscales = wpool.tile([P, 16 * P], U8, name="wscales", align_bytes=64)
+        gw_f = gw[:].bitcast(F32).rearrange("q (m n u) -> q m n u", m=16, n=P, u=2)
+        wx_f = wx[:].bitcast(F32)
+        wo_f = wo[:].bitcast(F32)
+        wr_f = wr[:].bitcast(F32)
+
+        def w_words(c, j, u):
+            if c < 2:
+                lo = j * 512 + 256 * c + P * u
+                return wx_f[:, lo : lo + P]
+            lo = j * 256 + P * u
+            return (wo_f if c == 2 else wr_f)[:, lo : lo + P]
+
+        def w_slot(c, j):
+            return PASS_ORDER.index(c) * 4 + j
+
+        for ci, c in enumerate(PASS_ORDER):
+            for jj in range(2):
+                pt = tx_bank("wt")
+                ptv = pt[:].rearrange("q (m u n) -> q m u n", m=2, u=2, n=P)
+                for m2 in range(2):
+                    for u in range(2):
+                        nc.tensor.transpose(ptv[:, m2, u, :], w_words(c, 2 * jj + m2, u), ident[:])
+                s0 = w_slot(c, 2 * jj)
+                dst = gw_f[:, s0 : s0 + 2, :, :]
+                srcv = ptv.rearrange("q m u n -> q m n u")
+                if jj == 0:
+                    nc.scalar.copy(out=dst, in_=srcv)
+                else:
+                    nc.vector.tensor_copy(out=dst, in_=srcv)
+            nc.vector.quantize_mx(
+                out=wcodes[:, ci * 512 : (ci + 1) * 512].bitcast(FP8X4),
+                scales=wscales[:, ci * 512 : (ci + 1) * 512],
+                in_=gw[:, ci * 2048 : (ci + 1) * 2048],
+            )
+
+        quant = {}
+        etile = {}
+
+        def stage_a(g):
+            xs, ss, bs, ms = loaded[g]
+            xs_f = xs[:].bitcast(F32).rearrange("p (t w) -> p t w", t=4)
+            ss_f = ss[:].bitcast(F32).rearrange("p (t w) -> p t w", t=4)
+            bs_f = bs[:].bitcast(F32).rearrange("p (t w) -> p t w", t=4)
+            ms_f = ms[:].bitcast(F32).rearrange("p (t w) -> p t w", t=4)
+            codes = {}
+            grs = {}
+            n_copy = 0
+            for c in PASS_ORDER:
+                src_f = xs_f if c < 2 else ss_f
+                woff = 256 * (c % 2)
+                gr = qp.tile([P, 4 * GS], BF16, name="gr%d" % c, tag="gr%d" % c, align_bytes=64)
+                gr_f = gr[:].bitcast(F32).rearrange("q (h t i u) -> q h t i u", h=2, t=2, i=P, u=2)
+                for h in range(2):
+                    pt = tx_bank("xt")
+                    ptv = pt[:].rearrange("q (t u i) -> q t u i", t=2, u=2, i=P)
+                    for t2 in range(2):
+                        for u in range(2):
+                            nc.tensor.transpose(
+                                ptv[:, t2, u, :], src_f[:, 2 * h + t2, woff + P * u : woff + P * u + P], ident[:]
+                            )
+                    srcv = ptv.rearrange("q t u i -> q t i u")
+                    if n_copy in TX_ON_VECTOR:
+                        nc.vector.tensor_copy(out=gr_f[:, h], in_=srcv)
+                    else:
+                        nc.scalar.copy(out=gr_f[:, h], in_=srcv)
+                    n_copy += 1
+                ac = qp.tile([P, GS], U32, name="ac%d" % c, tag="ac%d" % c, align_bytes=64)
+                asc = qp.tile([P, GS], U8, name="as%d" % c, tag="as%d" % c, align_bytes=64)
+                nc.vector.quantize_mx(out=ac[:].bitcast(FP8X4), scales=asc[:], in_=gr[:])
+                codes[c] = (ac, asc)
+                grs[c] = gr
+            quant[g] = codes
+            spk4 = grs[3][:].rearrange("q (s t) -> q s t", t=4)
+
+            es = []
+            for u in range(2):
+                pb = ps.tile([P, 512], F32, name="pb", tag="tm", bufs=2)
+                pbv = pb[:].rearrange("q (t i) -> q t i", t=4)
+                for t in range(4):
+                    nc.tensor.transpose(pbv[:, t, :], bs_f[:, t, P * u : P * u + P], ident[:])
+                pm = ps.tile([P, 512], F32, name="pm", tag="tm", bufs=2)
+                pmv = pm[:].rearrange("q (t i) -> q t i", t=4)
+                for t in range(4):
+                    nc.tensor.transpose(pmv[:, t, :], ms_f[:, t, P * u : P * u + P], ident[:])
+                bt2 = pb[:].bitcast(BF16).rearrange("q (s e) -> q s e", e=2)
+                mem2 = pm[:].bitcast(BF16).rearrange("q (s e) -> q s e", e=2)
+                for e in range(2):
+                    j = 2 * u + e
+                    jc = slice(j, j + 1)
+                    spkv = spk4[:, :, j]
+                    yt = ep.tile([P, GS], F32, name="yt", tag="yt", bufs=6)
+                    mt = ep.tile([P, GS], F32, name="mt", tag="mt", bufs=12)
+                    nc.scalar.activation(out=yt[:], in_=spkv, func=ACT.Identity, bias=0.1, scale=qq[:, jc])
+                    nc.vector.scalar_tensor_tensor(
+                        out=yt[:], in0=bt2[:, :, e], scalar=pq[:, jc], in1=yt[:], op0=ALU.mult, op1=ALU.add
+                    )
+                    nc.scalar.activation(out=mt[:], in_=mem2[:, :, e], func=ACT.Identity, bias=k0[:, jc], scale=aa[:, jc])
+                    eng = nc.gpsimd if j in Y3_ON_GPSIMD else nc.vector
+                    eng.tensor_tensor(out=yt[:], in0=yt[:], in1=spkv, op=ALU.mult)
+                    eng = nc.gpsimd if j in E_ON_GPSIMD else nc.vector
+                    eng.tensor_tensor(out=mt[:], in0=mt[:], in1=yt[:], op=ALU.subtract)
+                    es.append(mt)
+            etile[g] = es
+
+        def stage_b(g):
+            codes = quant[g]
+            for j in range(4):
+                acc = ps.tile([P, GS], F32, name="acc", tag="mx", bufs=2)
+                for ci, c in enumerate(PASS_ORDER):
+                    ac, asc = codes[c]
+                    s0 = w_slot(c, j) * P
+                    nc.tensor.matmul_mx(
+                        out=acc[:],
+                        lhsT=wcodes[:, s0 : s0 + P].bitcast(FP8X4),
+                        lhsT_scale=wscales[:, s0 : s0 + P],
+                        rhs=ac[:].bitcast(FP8X4),
+                        rhs_scale=asc[:],
+                        start=(ci == 0),
+                        stop=(ci == 3),
+                    )
+                mt = etile[g][j]
+                nc.vector.scalar_tensor_tensor(
+                    out=mt[:], in0=acc[:], scalar=c3[:, j : j + 1], in1=mt[:], op0=ALU.mult, op1=ALU.add
+                )
+
+        def stage_c(g):
+            es = etile[g]
+            ob = ep.tile([P, 4 * R_IN], F32, name="ob", tag="ob", bufs=2)
+            obv = ob[:].rearrange("i (t u q e) -> i t u q e", t=4, u=2, q=P, e=2)
+            for t in range(4):
+                bk = ps.tile([P, 512], F32, name="bk", tag="bk", bufs=1)
+                bkv = bk[:].rearrange("i (j q) -> i j q", j=4)
+                for j in range(4):
+                    nc.tensor.transpose(bkv[:, j, :], es[j][:, t * P : (t + 1) * P], ident[:])
+                srcv = bk[:].rearrange("i (u e q) -> i u q e", u=2, e=2, q=P)
+                if t in FINAL_ON_VECTOR:
+                    nc.vector.tensor_copy(out=obv[:, t], in_=srcv)
+                else:
+                    nc.scalar.copy(out=obv[:, t], in_=srcv)
+            nc.sync.dma_start(
+                out=out[g * GS : (g + 1) * GS, :].rearrange("(p t) n -> p t n", t=4),
+                in_=ob[:].rearrange("p (t n) -> p t n", t=4),
+            )
+
+        for it in range(G + 2):
+            if it + 2 < G:
+                load(it + 2)
+            if it < G:
+                stage_a(it)
+            if 0 <= it - 1 < G:
+                stage_b(it - 1)
+            if 0 <= it - 2 < G:
+                stage_c(it - 2)

@@ -13,67 +13,87 @@ ACT = mybir.ActivationFunctionType
 
 P = 128
 B, IN_DIM, R_IN = 4096, 1024, 512
-GS = 512
-G = B // GS
 FLOPS = 2 * B * (IN_DIM + 2 * R_IN) * R_IN
 
+NTS = (1, 1, 2, 4, 4, 4, 4, 4, 4, 2, 1, 1)
+G = len(NTS)
 PASS_ORDER = (3, 2, 0, 1)
-TX_ON_VECTOR = (2, 6)
-Y3_ON_GPSIMD = ()
-E_ON_GPSIMD = (0, 1, 2, 3)
-FINAL_ON_VECTOR = ()
+OFF_Y1 = (0, 2)
+OFF_BT = (1, 3)
+OFF_MEM = (4, 6)
+OFF_Q = 1
+OFF_MX = 6
+OFF_BK = 11
+N_UNITS = 4 * G + OFF_BK + 4
+PINNED = True
+assert sum(NTS) * P == B
+
+
+def unit_of(n, off):
+    d = n - off
+    if d >= 0 and d // 4 < G:
+        return (d // 4, d % 4)
+    return None
+
+
+def halves_of(n, offs):
+    res = []
+    for u in range(2):
+        d = n - offs[u]
+        if d >= 0 and d % 4 == 0 and d // 4 < G:
+            res.append((d // 4, u))
+    return res
 
 
 def tile_snnlayer_pa_t_kernel(
     tc, x_t, spk_t, mem_t_in, b_t_in, W_x2in, b_x2in, W_rec4in, b_rec4in, W_out2in, b_out2in, tau_adp_in, tau_m_in, out
 ):
     nc = tc.nc
+    base = [P * sum(NTS[:g]) for g in range(G)]
     with ExitStack() as ctx:
+        if PINNED:
+            ctx.enter_context(tc.manual_schedule())
         const = ctx.enter_context(tc.tile_pool(name="const", bufs=1))
-        wpool = ctx.enter_context(tc.tile_pool(name="wpool", bufs=1))
         ld = ctx.enter_context(tc.tile_pool(name="ld", bufs=3))
         qp = ctx.enter_context(tc.tile_pool(name="qp", bufs=2))
         ep = ctx.enter_context(tc.tile_pool(name="ep", bufs=2))
         ps = ctx.enter_context(tc.psum_pool(name="ps", bufs=1))
 
-        def tx_bank(name):
-            return ps.tile([P, 512], F32, name=name, tag="tx", bufs=3)
+        def bank(name, tag, bufs):
+            return ps.tile([P, 512], F32, name=name, tag=tag, bufs=bufs)
 
+        srcs = {"ss": (spk_t, 1024), "xs": (x_t, 1024), "bs": (b_t_in, 512), "ms": (mem_t_in, 512)}
         loaded = {}
 
-        def load(g):
-            rows = slice(g * GS, (g + 1) * GS)
-            ss = ld.tile([P, 4 * 1024], BF16, name="ss", tag="ss")
-            xs = ld.tile([P, 4 * 1024], BF16, name="xs", tag="xs")
-            bs = ld.tile([P, 4 * 512], BF16, name="bs", tag="bs")
-            ms = ld.tile([P, 4 * 512], BF16, name="ms", tag="ms")
-            for dst, src in ((ss, spk_t), (xs, x_t), (bs, b_t_in), (ms, mem_t_in)):
+        def load(g, names):
+            if g >= G:
+                return
+            nt = NTS[g]
+            for nm in names:
+                src, width = srcs[nm]
+                dst = ld.tile([P, 4 * width], BF16, name=nm, tag=nm)
                 nc.sync.dma_start(
-                    out=dst[:].rearrange("p (t k) -> p t k", t=4),
-                    in_=src[rows, :].rearrange("(p t) k -> p t k", t=4),
+                    out=dst[:, 0 : nt * width].rearrange("p (t k) -> p t k", t=nt),
+                    in_=src[base[g] : base[g] + nt * P, :].rearrange("(p t) k -> p t k", t=nt),
                 )
-            loaded[g] = (xs, ss, bs, ms)
-
-        ident = const.tile([P, P], F32, name="ident")
-        make_identity(nc, ident[:])
+                loaded[(g, nm)] = dst
 
         craw = const.tile([P, 256], BF16, name="craw")
         nc.vector.memset(craw[:], 0.0)
         for v, vec in enumerate((b_x2in, b_rec4in, b_out2in, tau_adp_in, tau_m_in)):
-            nc.scalar.dma_start(out=craw[2 * v : 2 * v + 2, :], in_=vec.rearrange("(u w) -> u w", u=2))
+            nc.sync.dma_start(out=craw[2 * v : 2 * v + 2, :], in_=vec.rearrange("(u w) -> u w", u=2))
+        ident = const.tile([P, P], F32, name="ident")
+        make_identity(nc, ident[:])
 
-        load(0)
-        wx = wpool.tile([P, 4 * 1024], BF16, name="wx")
-        wo = wpool.tile([P, 4 * 512], BF16, name="wo")
-        wr = wpool.tile([P, 4 * 512], BF16, name="wr")
-        for dst, src in ((wr, W_rec4in), (wo, W_out2in), (wx, W_x2in)):
+        wro = ld.tile([P, 4096], BF16, name="wro", tag="ss")
+        wx = ld.tile([P, 4096], BF16, name="wx", tag="xs")
+        for dst, src in ((wro[:, 0:2048], W_rec4in), (wro[:, 2048:4096], W_out2in), (wx[:], W_x2in)):
             nc.sync.dma_start(
-                out=dst[:].rearrange("p (u e k) -> p u e k", u=2, e=2),
+                out=dst.rearrange("p (u e k) -> p u e k", u=2, e=2),
                 in_=src.rearrange("(u p e) k -> p u e k", u=2, p=P, e=2),
             )
-        load(1)
 
-        cps = tx_bank("cps")
+        cps = bank("cps", "tx", 4)
         nc.tensor.transpose(cps[:, 0:P], craw[:].bitcast(F32), ident[:])
         cst = const.tile([P, 20], F32, name="cst")
         nc.vector.tensor_copy(out=cst[:], in_=cps[:].bitcast(BF16)[:, 0:20])
@@ -88,165 +108,209 @@ def tile_snnlayer_pa_t_kernel(
         qq = const.tile([P, 4], F32, name="qq")
         c3 = const.tile([P, 4], F32, name="c3")
         k0 = const.tile([P, 4], F32, name="k0")
-        nc.vector.tensor_scalar_mul(out=pq[:], in0=sg[:, 0:4], scalar1=1.8)
-        nc.vector.tensor_scalar_mul(out=qq[:], in0=ng[:, 0:4], scalar1=1.8)
-        nc.vector.tensor_scalar_mul(out=c3[:], in0=ng[:, 4:8], scalar1=3.0)
-        nc.vector.tensor_mul(out=k0[:], in0=c3[:], in1=bsum[:])
+        nc.scalar.mul(out=qq[:], in_=ng[:, 0:4], mul=1.8)
+        nc.scalar.mul(out=pq[:], in_=sg[:, 0:4], mul=1.8)
+        nc.scalar.mul(out=c3[:], in_=ng[:, 4:8], mul=3.0)
         aa = sg[:, 4:8]
 
-        gw = wpool.tile([P, 16 * 512], BF16, name="gw", align_bytes=64)
-        wcodes = wpool.tile([P, 16 * P], U32, name="wcodes", align_bytes=64)
-        wscales = wpool.tile([P, 16 * P], U8, name="wscales", align_bytes=64)
-        gw_f = gw[:].bitcast(F32).rearrange("q (m n u) -> q m n u", m=16, n=P, u=2)
+        wcodes = const.tile([P, 16 * P], U32, name="wcodes", align_bytes=64)
+        wscales = const.tile([P, 16 * P], U8, name="wscales", align_bytes=64)
         wx_f = wx[:].bitcast(F32)
-        wo_f = wo[:].bitcast(F32)
-        wr_f = wr[:].bitcast(F32)
+        wro_f = wro[:].bitcast(F32)
 
         def w_words(c, j, u):
             if c < 2:
                 lo = j * 512 + 256 * c + P * u
                 return wx_f[:, lo : lo + P]
-            lo = j * 256 + P * u
-            return (wo_f if c == 2 else wr_f)[:, lo : lo + P]
+            lo = (0 if c == 3 else 1024) + j * 256 + P * u
+            return wro_f[:, lo : lo + P]
 
-        def w_slot(c, j):
-            return PASS_ORDER.index(c) * 4 + j
+        gr = {}
+        ac = {}
+        yts = {}
+        mts = {}
+        tmb = {}
+        mx_at = {}
+        gws = {}
 
+        def w_quantise(ci):
+            nc.vector.quantize_mx(
+                out=wcodes[:, ci * 512 : (ci + 1) * 512].bitcast(FP8X4),
+                scales=wscales[:, ci * 512 : (ci + 1) * 512],
+                in_=gws[ci][:],
+            )
+
+        load(0, ("ss", "xs", "bs", "ms"))
+        load(1, ("ss", "xs", "bs", "ms"))
         for ci, c in enumerate(PASS_ORDER):
+            gw = qp.tile([P, 2048], BF16, name="gw%d" % c, tag="gr%d" % c, align_bytes=64)
+            gws[ci] = gw
+            gw_f = gw[:].bitcast(F32).rearrange("q (m n u) -> q m n u", m=4, n=P, u=2)
             for jj in range(2):
-                pt = tx_bank("wt")
+                pt = bank("wt", "tx", 4)
                 ptv = pt[:].rearrange("q (m u n) -> q m u n", m=2, u=2, n=P)
                 for m2 in range(2):
                     for u in range(2):
                         nc.tensor.transpose(ptv[:, m2, u, :], w_words(c, 2 * jj + m2, u), ident[:])
-                s0 = w_slot(c, 2 * jj)
-                dst = gw_f[:, s0 : s0 + 2, :, :]
+                dst = gw_f[:, 2 * jj : 2 * jj + 2, :, :]
                 srcv = ptv.rearrange("q m u n -> q m n u")
                 if jj == 0:
                     nc.scalar.copy(out=dst, in_=srcv)
                 else:
                     nc.vector.tensor_copy(out=dst, in_=srcv)
-            nc.vector.quantize_mx(
-                out=wcodes[:, ci * 512 : (ci + 1) * 512].bitcast(FP8X4),
-                scales=wscales[:, ci * 512 : (ci + 1) * 512],
-                in_=gw[:, ci * 2048 : (ci + 1) * 2048],
-            )
+            if ci == 0:
+                nc.vector.tensor_mul(out=k0[:], in0=c3[:], in1=bsum[:])
+            else:
+                w_quantise(ci - 1)
+        w_quantise(3)
+        load(2, ("ss", "xs", "bs", "ms"))
 
-        quant = {}
-        etile = {}
+        def quantises(n):
+            q = unit_of(n, OFF_Q)
+            if q is not None:
+                g, r = q
+                c = PASS_ORDER[r]
+                ns = P * NTS[g]
+                a_c = qp.tile([P, 512], U32, name="ac%d" % c, tag="ac%d" % c, bufs=3, align_bytes=64)
+                a_s = qp.tile([P, 512], U8, name="as%d" % c, tag="as%d" % c, bufs=3, align_bytes=64)
+                nc.vector.quantize_mx(out=a_c[:, 0:ns].bitcast(FP8X4), scales=a_s[:, 0:ns], in_=gr[(g, c)][:, 0 : 4 * ns])
+                ac[(g, c)] = (a_c, a_s)
 
-        def stage_a(g):
-            xs, ss, bs, ms = loaded[g]
-            xs_f = xs[:].bitcast(F32).rearrange("p (t w) -> p t w", t=4)
-            ss_f = ss[:].bitcast(F32).rearrange("p (t w) -> p t w", t=4)
-            bs_f = bs[:].bitcast(F32).rearrange("p (t w) -> p t w", t=4)
-            ms_f = ms[:].bitcast(F32).rearrange("p (t w) -> p t w", t=4)
-            codes = {}
-            grs = {}
-            n_copy = 0
-            for c in PASS_ORDER:
-                src_f = xs_f if c < 2 else ss_f
+        for n in range(N_UNITS):
+            if n % 4 == 0 and n > 0:
+                load(n // 4 + 2, ("ss", "xs"))
+            elif n % 4 == 3 and n > 3:
+                load(n // 4 + 2, ("bs", "ms"))
+
+            s_copies = []
+            a = unit_of(n, 0)
+            if a is not None:
+                g, r = a
+                c = PASS_ORDER[r]
+                nt = NTS[g]
+                tf = min(nt, 2)
+                nf = nt // tf
+                src_t = loaded[(g, "xs" if c < 2 else "ss")]
+                src_f = src_t[:].bitcast(F32)[:, 0 : nt * 512].rearrange("p (t w) -> p t w", t=nt)
                 woff = 256 * (c % 2)
-                gr = qp.tile([P, 4 * GS], BF16, name="gr%d" % c, tag="gr%d" % c, align_bytes=64)
-                gr_f = gr[:].bitcast(F32).rearrange("q (h t i u) -> q h t i u", h=2, t=2, i=P, u=2)
-                for h in range(2):
-                    pt = tx_bank("xt")
-                    ptv = pt[:].rearrange("q (t u i) -> q t u i", t=2, u=2, i=P)
-                    for t2 in range(2):
+                grt = qp.tile([P, 2048], BF16, name="gr%d" % c, tag="gr%d" % c, align_bytes=64)
+                gr[(g, c)] = grt
+                gr_f = grt[:].bitcast(F32)[:, 0 : nt * 256].rearrange("q (h t i u) -> q h t i u", h=nf, t=tf, i=P, u=2)
+                for h in range(nf):
+                    pt = bank("xt", "tx", 4)
+                    ptv = pt[:, 0 : tf * 256].rearrange("q (t u i) -> q t u i", t=tf, u=2, i=P)
+                    for t2 in range(tf):
                         for u in range(2):
                             nc.tensor.transpose(
-                                ptv[:, t2, u, :], src_f[:, 2 * h + t2, woff + P * u : woff + P * u + P], ident[:]
+                                ptv[:, t2, u, :], src_f[:, tf * h + t2, woff + P * u : woff + P * u + P], ident[:]
                             )
-                    srcv = ptv.rearrange("q t u i -> q t i u")
-                    if n_copy in TX_ON_VECTOR:
-                        nc.vector.tensor_copy(out=gr_f[:, h], in_=srcv)
-                    else:
-                        nc.scalar.copy(out=gr_f[:, h], in_=srcv)
-                    n_copy += 1
-                ac = qp.tile([P, GS], U32, name="ac%d" % c, tag="ac%d" % c, align_bytes=64)
-                asc = qp.tile([P, GS], U8, name="as%d" % c, tag="as%d" % c, align_bytes=64)
-                nc.vector.quantize_mx(out=ac[:].bitcast(FP8X4), scales=asc[:], in_=gr[:])
-                codes[c] = (ac, asc)
-                grs[c] = gr
-            quant[g] = codes
-            spk4 = grs[3][:].rearrange("q (s t) -> q s t", t=4)
+                    s_copies.append((gr_f[:, h], ptv.rearrange("q t u i -> q t i u")))
+            bt_now = halves_of(n, OFF_BT)
+            mem_now = halves_of(n, OFF_MEM)
+            for kind, nm, lst in (("b", "bs", bt_now), ("m", "ms", mem_now)):
+                for g, u in lst:
+                    nt = NTS[g]
+                    src_f = loaded[(g, nm)][:].bitcast(F32)[:, 0 : nt * 256].rearrange("p (t w) -> p t w", t=nt)
+                    pb = bank("p" + kind, "tm", 2)
+                    pbv = pb[:, 0 : nt * P].rearrange("q (t i) -> q t i", t=nt)
+                    for t in range(nt):
+                        nc.tensor.transpose(pbv[:, t, :], src_f[:, t, P * u : P * u + P], ident[:])
+                    tmb[(g, kind, u)] = pb[:].bitcast(BF16)[:, 0 : 2 * nt * P].rearrange("q (s e) -> q s e", e=2)
+            k = unit_of(n, OFF_BK)
+            bk = None
+            if k is not None and k[1] < NTS[k[0]]:
+                g, t = k
+                bk = bank("bk", "tx", 4)
+                bkv = bk[:].rearrange("i (j q) -> i j q", j=4)
+                for j in range(4):
+                    nc.tensor.transpose(bkv[:, j, :], mts[(g, j)][:, t * P : (t + 1) * P], ident[:])
 
-            es = []
-            for u in range(2):
-                pb = ps.tile([P, 512], F32, name="pb", tag="tm", bufs=2)
-                pbv = pb[:].rearrange("q (t i) -> q t i", t=4)
-                for t in range(4):
-                    nc.tensor.transpose(pbv[:, t, :], bs_f[:, t, P * u : P * u + P], ident[:])
-                pm = ps.tile([P, 512], F32, name="pm", tag="tm", bufs=2)
-                pmv = pm[:].rearrange("q (t i) -> q t i", t=4)
-                for t in range(4):
-                    nc.tensor.transpose(pmv[:, t, :], ms_f[:, t, P * u : P * u + P], ident[:])
-                bt2 = pb[:].bitcast(BF16).rearrange("q (s e) -> q s e", e=2)
-                mem2 = pm[:].bitcast(BF16).rearrange("q (s e) -> q s e", e=2)
+            for dst, srcv in s_copies:
+                nc.scalar.copy(out=dst, in_=srcv)
+            if bk is not None:
+                g, t = k
+                nt = NTS[g]
+                ob = ep.tile([P, R_IN], F32, name="ob", tag="ob", bufs=8)
+                nc.scalar.copy(
+                    out=ob[:].rearrange("i (u q e) -> i u q e", u=2, q=P, e=2),
+                    in_=bk[:].rearrange("i (u e q) -> i u q e", u=2, e=2, q=P),
+                )
+                nc.sync.dma_start(
+                    out=out[base[g] : base[g] + nt * P, :].rearrange("(p t) n -> p t n", t=nt)[:, t, :], in_=ob[:]
+                )
+            for g, u in halves_of(n, OFF_Y1):
+                ns = P * NTS[g]
+                spk4 = gr[(g, 3)][:, 0 : 4 * ns].rearrange("q (s t) -> q s t", t=4)
+                for j in (2 * u, 2 * u + 1):
+                    yt = ep.tile([P, 512], F32, name="yt", tag="yt", bufs=8)
+                    yts[(g, j)] = yt
+                    nc.scalar.activation(
+                        out=yt[:, 0:ns], in_=spk4[:, :, j], func=ACT.Identity, bias=0.1, scale=qq[:, j : j + 1]
+                    )
+
+            prev = mx_at.get(n - 1)
+            if prev is not None:
+                g, j, acc = prev
+                ns = P * NTS[g]
+                mt = mts[(g, j)]
+                nc.vector.scalar_tensor_tensor(
+                    out=mt[:, 0:ns], in0=acc[:, 0:ns], scalar=c3[:, j : j + 1], in1=mt[:, 0:ns], op0=ALU.mult, op1=ALU.add
+                )
+            if bt_now:
+                quantises(n)
+            for g, u in mem_now:
+                ns = P * NTS[g]
                 for e in range(2):
                     j = 2 * u + e
-                    jc = slice(j, j + 1)
-                    spkv = spk4[:, :, j]
-                    yt = ep.tile([P, GS], F32, name="yt", tag="yt", bufs=6)
-                    mt = ep.tile([P, GS], F32, name="mt", tag="mt", bufs=12)
-                    nc.scalar.activation(out=yt[:], in_=spkv, func=ACT.Identity, bias=0.1, scale=qq[:, jc])
+                    mt = ep.tile([P, 512], F32, name="mt", tag="mt", bufs=14)
+                    mts[(g, j)] = mt
                     nc.vector.scalar_tensor_tensor(
-                        out=yt[:], in0=bt2[:, :, e], scalar=pq[:, jc], in1=yt[:], op0=ALU.mult, op1=ALU.add
+                        out=mt[:, 0:ns],
+                        in0=tmb[(g, "m", u)][:, :, e],
+                        scalar=aa[:, j : j + 1],
+                        in1=yts[(g, j)][:, 0:ns],
+                        op0=ALU.mult,
+                        op1=ALU.add,
                     )
-                    nc.scalar.activation(out=mt[:], in_=mem2[:, :, e], func=ACT.Identity, bias=k0[:, jc], scale=aa[:, jc])
-                    eng = nc.gpsimd if j in Y3_ON_GPSIMD else nc.vector
-                    eng.tensor_tensor(out=yt[:], in0=yt[:], in1=spkv, op=ALU.mult)
-                    eng = nc.gpsimd if j in E_ON_GPSIMD else nc.vector
-                    eng.tensor_tensor(out=mt[:], in0=mt[:], in1=yt[:], op=ALU.subtract)
-                    es.append(mt)
-            etile[g] = es
+            for g, u in bt_now:
+                ns = P * NTS[g]
+                spk4 = gr[(g, 3)][:, 0 : 4 * ns].rearrange("q (s t) -> q s t", t=4)
+                for e in range(2):
+                    j = 2 * u + e
+                    yt = yts[(g, j)]
+                    nc.vector.scalar_tensor_tensor(
+                        out=yt[:, 0:ns],
+                        in0=tmb[(g, "b", u)][:, :, e],
+                        scalar=pq[:, j : j + 1],
+                        in1=yt[:, 0:ns],
+                        op0=ALU.mult,
+                        op1=ALU.add,
+                    )
+                for e in range(2):
+                    j = 2 * u + e
+                    yt = yts[(g, j)]
+                    nc.gpsimd.tensor_tensor(out=yt[:, 0:ns], in0=yt[:, 0:ns], in1=spk4[:, :, j], op=ALU.mult)
+                    nc.gpsimd.tensor_scalar(
+                        out=yt[:, 0:ns], in0=yt[:, 0:ns], scalar1=-1.0, scalar2=k0[:, j : j + 1], op0=ALU.mult, op1=ALU.add
+                    )
+            if not bt_now:
+                quantises(n)
 
-        def stage_b(g):
-            codes = quant[g]
-            for j in range(4):
-                acc = ps.tile([P, GS], F32, name="acc", tag="mx", bufs=2)
+            m = unit_of(n, OFF_MX)
+            if m is not None:
+                g, j = m
+                ns = P * NTS[g]
+                acc = bank("acc", "mx", 2)
                 for ci, c in enumerate(PASS_ORDER):
-                    ac, asc = codes[c]
-                    s0 = w_slot(c, j) * P
+                    a_c, a_s = ac[(g, c)]
+                    s0 = (ci * 4 + j) * P
                     nc.tensor.matmul_mx(
-                        out=acc[:],
+                        out=acc[:, 0:ns],
                         lhsT=wcodes[:, s0 : s0 + P].bitcast(FP8X4),
                         lhsT_scale=wscales[:, s0 : s0 + P],
-                        rhs=ac[:].bitcast(FP8X4),
-                        rhs_scale=asc[:],
+                        rhs=a_c[:, 0:ns].bitcast(FP8X4),
+                        rhs_scale=a_s[:, 0:ns],
                         start=(ci == 0),
                         stop=(ci == 3),
                     )
-                mt = etile[g][j]
-                nc.vector.scalar_tensor_tensor(
-                    out=mt[:], in0=acc[:], scalar=c3[:, j : j + 1], in1=mt[:], op0=ALU.mult, op1=ALU.add
-                )
-
-        def stage_c(g):
-            es = etile[g]
-            ob = ep.tile([P, 4 * R_IN], F32, name="ob", tag="ob", bufs=2)
-            obv = ob[:].rearrange("i (t u q e) -> i t u q e", t=4, u=2, q=P, e=2)
-            for t in range(4):
-                bk = ps.tile([P, 512], F32, name="bk", tag="bk", bufs=1)
-                bkv = bk[:].rearrange("i (j q) -> i j q", j=4)
-                for j in range(4):
-                    nc.tensor.transpose(bkv[:, j, :], es[j][:, t * P : (t + 1) * P], ident[:])
-                srcv = bk[:].rearrange("i (u e q) -> i u q e", u=2, e=2, q=P)
-                if t in FINAL_ON_VECTOR:
-                    nc.vector.tensor_copy(out=obv[:, t], in_=srcv)
-                else:
-                    nc.scalar.copy(out=obv[:, t], in_=srcv)
-            nc.sync.dma_start(
-                out=out[g * GS : (g + 1) * GS, :].rearrange("(p t) n -> p t n", t=4),
-                in_=ob[:].rearrange("p (t n) -> p t n", t=4),
-            )
-
-        for it in range(G + 2):
-            if it + 2 < G:
-                load(it + 2)
-            if it < G:
-                stage_a(it)
-            if 0 <= it - 1 < G:
-                stage_b(it - 1)
-            if 0 <= it - 2 < G:
-                stage_c(it - 2)
+                mx_at[n] = (g, j, acc)

@@ -176,6 +176,22 @@ def tile_snnlayer_pa_t_kernel(
                 nc.vector.quantize_mx(out=a_c[:, 0:ns].bitcast(FP8X4), scales=a_s[:, 0:ns], in_=gr[(g, c)][:, 0 : 4 * ns])
                 ac[(g, c)] = (a_c, a_s)
 
+        def mx_passes(n, which):
+            g, j, acc = mx_at[n]
+            ns = P * NTS[g]
+            for ci in which:
+                a_c, a_s = ac[(g, PASS_ORDER[ci])]
+                s0 = (ci * 4 + j) * P
+                nc.tensor.matmul_mx(
+                    out=acc[:, 0:ns],
+                    lhsT=wcodes[:, s0 : s0 + P].bitcast(FP8X4),
+                    lhsT_scale=wscales[:, s0 : s0 + P],
+                    rhs=a_c[:, 0:ns].bitcast(FP8X4),
+                    rhs_scale=a_s[:, 0:ns],
+                    start=(ci == 0),
+                    stop=(ci == 3),
+                )
+
         for n in range(N_UNITS):
             if n % 4 == 0 and n > 0:
                 load(n // 4 + 2, ("ss", "xs"))
@@ -205,6 +221,10 @@ def tile_snnlayer_pa_t_kernel(
                                 ptv[:, t2, u, :], src_f[:, tf * h + t2, woff + P * u : woff + P * u + P], ident[:]
                             )
                     s_copies.append((gr_f[:, h], ptv.rearrange("q t u i -> q t i u")))
+            m = unit_of(n, OFF_MX)
+            if m is not None:
+                mx_at[n] = (m[0], m[1], bank("acc", "mx", 2))
+                mx_passes(n, (0, 1))
             bt_now = halves_of(n, OFF_BT)
             mem_now = halves_of(n, OFF_MEM)
             for kind, nm, lst in (("b", "bs", bt_now), ("m", "ms", mem_now)):
@@ -224,6 +244,9 @@ def tile_snnlayer_pa_t_kernel(
                 bkv = bk[:].rearrange("i (j q) -> i j q", j=4)
                 for j in range(4):
                     nc.tensor.transpose(bkv[:, j, :], mts[(g, j)][:, t * P : (t + 1) * P], ident[:])
+
+            if m is not None:
+                mx_passes(n, (2, 3))
 
             for dst, srcv in s_copies:
                 nc.scalar.copy(out=dst, in_=srcv)
@@ -295,22 +318,3 @@ def tile_snnlayer_pa_t_kernel(
                     )
             if not bt_now:
                 quantises(n)
-
-            m = unit_of(n, OFF_MX)
-            if m is not None:
-                g, j = m
-                ns = P * NTS[g]
-                acc = bank("acc", "mx", 2)
-                for ci, c in enumerate(PASS_ORDER):
-                    a_c, a_s = ac[(g, c)]
-                    s0 = (ci * 4 + j) * P
-                    nc.tensor.matmul_mx(
-                        out=acc[:, 0:ns],
-                        lhsT=wcodes[:, s0 : s0 + P].bitcast(FP8X4),
-                        lhsT_scale=wscales[:, s0 : s0 + P],
-                        rhs=a_c[:, 0:ns].bitcast(FP8X4),
-                        rhs_scale=a_s[:, 0:ns],
-                        start=(ci == 0),
-                        stop=(ci == 3),
-                    )
-                mx_at[n] = (g, j, acc)

@@ -21,9 +21,9 @@ PASS_ORDER = (3, 2, 0, 1)
 OFF_Y1 = (0, 2)
 OFF_BT = (1, 3)
 OFF_MEM = (4, 6)
-OFF_Q = 1
-OFF_MX = 6
-OFF_BK = 11
+OFF_QP = (3, 5)
+OFF_MX = 7
+OFF_BK = 12
 N_UNITS = 4 * G + OFF_BK + 4
 PINNED = True
 assert sum(NTS) * P == B
@@ -133,26 +133,27 @@ def tile_snnlayer_pa_t_kernel(
         mx_at = {}
         gws = {}
 
-        def w_quantise(ci):
+        def w_quantise(pi):
             nc.vector.quantize_mx(
-                out=wcodes[:, ci * 512 : (ci + 1) * 512].bitcast(FP8X4),
-                scales=wscales[:, ci * 512 : (ci + 1) * 512],
-                in_=gws[ci][:],
+                out=wcodes[:, pi * 1024 : (pi + 1) * 1024].bitcast(FP8X4),
+                scales=wscales[:, pi * 1024 : (pi + 1) * 1024],
+                in_=gws[pi][:],
             )
 
         load(0, ("ss", "xs", "bs", "ms"))
         load(1, ("ss", "xs", "bs", "ms"))
         for ci, c in enumerate(PASS_ORDER):
-            gw = qp.tile([P, 2048], BF16, name="gw%d" % c, tag="gr%d" % c, align_bytes=64)
-            gws[ci] = gw
-            gw_f = gw[:].bitcast(F32).rearrange("q (m n u) -> q m n u", m=4, n=P, u=2)
+            if ci % 2 == 0:
+                gws[ci // 2] = qp.tile([P, 4096], BF16, name="gw%d" % (ci // 2), tag="gr%d" % (ci // 2), align_bytes=64)
+            gw_f = gws[ci // 2][:].bitcast(F32).rearrange("q (m n u) -> q m n u", m=8, n=P, u=2)
             for jj in range(2):
                 pt = bank("wt", "tx", 4)
                 ptv = pt[:].rearrange("q (m u n) -> q m u n", m=2, u=2, n=P)
                 for m2 in range(2):
                     for u in range(2):
                         nc.tensor.transpose(ptv[:, m2, u, :], w_words(c, 2 * jj + m2, u), ident[:])
-                dst = gw_f[:, 2 * jj : 2 * jj + 2, :, :]
+                m0 = 4 * (ci % 2) + 2 * jj
+                dst = gw_f[:, m0 : m0 + 2, :, :]
                 srcv = ptv.rearrange("q m u n -> q m n u")
                 if jj == 0:
                     nc.scalar.copy(out=dst, in_=srcv)
@@ -160,37 +161,20 @@ def tile_snnlayer_pa_t_kernel(
                     nc.vector.tensor_copy(out=dst, in_=srcv)
             if ci == 0:
                 nc.vector.tensor_mul(out=k0[:], in0=c3[:], in1=bsum[:])
-            else:
-                w_quantise(ci - 1)
-        w_quantise(3)
+            if ci == 2:
+                w_quantise(0)
+        w_quantise(1)
         load(2, ("ss", "xs", "bs", "ms"))
 
         def quantises(n):
-            q = unit_of(n, OFF_Q)
-            if q is not None:
-                g, r = q
-                c = PASS_ORDER[r]
+            for g, pi in halves_of(n, OFF_QP):
                 ns = P * NTS[g]
-                a_c = qp.tile([P, 512], U32, name="ac%d" % c, tag="ac%d" % c, bufs=3, align_bytes=64)
-                a_s = qp.tile([P, 512], U8, name="as%d" % c, tag="as%d" % c, bufs=3, align_bytes=64)
-                nc.vector.quantize_mx(out=a_c[:, 0:ns].bitcast(FP8X4), scales=a_s[:, 0:ns], in_=gr[(g, c)][:, 0 : 4 * ns])
-                ac[(g, c)] = (a_c, a_s)
-
-        def mx_passes(n, which):
-            g, j, acc = mx_at[n]
-            ns = P * NTS[g]
-            for ci in which:
-                a_c, a_s = ac[(g, PASS_ORDER[ci])]
-                s0 = (ci * 4 + j) * P
-                nc.tensor.matmul_mx(
-                    out=acc[:, 0:ns],
-                    lhsT=wcodes[:, s0 : s0 + P].bitcast(FP8X4),
-                    lhsT_scale=wscales[:, s0 : s0 + P],
-                    rhs=a_c[:, 0:ns].bitcast(FP8X4),
-                    rhs_scale=a_s[:, 0:ns],
-                    start=(ci == 0),
-                    stop=(ci == 3),
+                a_c = qp.tile([P, 1024], U32, name="ac%d" % pi, tag="ac%d" % pi, bufs=3, align_bytes=64)
+                a_s = qp.tile([P, 1024], U8, name="as%d" % pi, tag="as%d" % pi, bufs=3, align_bytes=64)
+                nc.vector.quantize_mx(
+                    out=a_c[:, 0 : 2 * ns].bitcast(FP8X4), scales=a_s[:, 0 : 2 * ns], in_=gr[(g, pi)][:, 0 : 8 * ns]
                 )
+                ac[(g, pi)] = (a_c, a_s)
 
         for n in range(N_UNITS):
             if n % 4 == 0 and n > 0:
@@ -209,9 +193,14 @@ def tile_snnlayer_pa_t_kernel(
                 src_t = loaded[(g, "xs" if c < 2 else "ss")]
                 src_f = src_t[:].bitcast(F32)[:, 0 : nt * 512].rearrange("p (t w) -> p t w", t=nt)
                 woff = 256 * (c % 2)
-                grt = qp.tile([P, 2048], BF16, name="gr%d" % c, tag="gr%d" % c, align_bytes=64)
-                gr[(g, c)] = grt
-                gr_f = grt[:].bitcast(F32)[:, 0 : nt * 256].rearrange("q (h t i u) -> q h t i u", h=nf, t=tf, i=P, u=2)
+                if r % 2 == 0:
+                    gr[(g, r // 2)] = qp.tile([P, 4096], BF16, name="gr%d" % (r // 2), tag="gr%d" % (r // 2), align_bytes=64)
+                w0 = (r % 2) * nt * 256
+                gr_f = (
+                    gr[(g, r // 2)][:]
+                    .bitcast(F32)[:, w0 : w0 + nt * 256]
+                    .rearrange("q (h t i u) -> q h t i u", h=nf, t=tf, i=P, u=2)
+                )
                 for h in range(nf):
                     pt = bank("xt", "tx", 4)
                     ptv = pt[:, 0 : tf * 256].rearrange("q (t u i) -> q t u i", t=tf, u=2, i=P)
@@ -221,10 +210,6 @@ def tile_snnlayer_pa_t_kernel(
                                 ptv[:, t2, u, :], src_f[:, tf * h + t2, woff + P * u : woff + P * u + P], ident[:]
                             )
                     s_copies.append((gr_f[:, h], ptv.rearrange("q t u i -> q t i u")))
-            m = unit_of(n, OFF_MX)
-            if m is not None:
-                mx_at[n] = (m[0], m[1], bank("acc", "mx", 2))
-                mx_passes(n, (0, 1))
             bt_now = halves_of(n, OFF_BT)
             mem_now = halves_of(n, OFF_MEM)
             for kind, nm, lst in (("b", "bs", bt_now), ("m", "ms", mem_now)):
@@ -245,9 +230,6 @@ def tile_snnlayer_pa_t_kernel(
                 for j in range(4):
                     nc.tensor.transpose(bkv[:, j, :], mts[(g, j)][:, t * P : (t + 1) * P], ident[:])
 
-            if m is not None:
-                mx_passes(n, (2, 3))
-
             for dst, srcv in s_copies:
                 nc.scalar.copy(out=dst, in_=srcv)
             if bk is not None:
@@ -263,7 +245,7 @@ def tile_snnlayer_pa_t_kernel(
                 )
             for g, u in halves_of(n, OFF_Y1):
                 ns = P * NTS[g]
-                spk4 = gr[(g, 3)][:, 0 : 4 * ns].rearrange("q (s t) -> q s t", t=4)
+                spk4 = gr[(g, 0)][:, 0 : 4 * ns].rearrange("q (s t) -> q s t", t=4)
                 for j in (2 * u, 2 * u + 1):
                     yt = ep.tile([P, 512], F32, name="yt", tag="yt", bufs=8)
                     yts[(g, j)] = yt
@@ -279,8 +261,7 @@ def tile_snnlayer_pa_t_kernel(
                 nc.vector.scalar_tensor_tensor(
                     out=mt[:, 0:ns], in0=acc[:, 0:ns], scalar=c3[:, j : j + 1], in1=mt[:, 0:ns], op0=ALU.mult, op1=ALU.add
                 )
-            if bt_now:
-                quantises(n)
+            quantises(n)
             for g, u in mem_now:
                 ns = P * NTS[g]
                 for e in range(2):
@@ -297,7 +278,7 @@ def tile_snnlayer_pa_t_kernel(
                     )
             for g, u in bt_now:
                 ns = P * NTS[g]
-                spk4 = gr[(g, 3)][:, 0 : 4 * ns].rearrange("q (s t) -> q s t", t=4)
+                spk4 = gr[(g, 0)][:, 0 : 4 * ns].rearrange("q (s t) -> q s t", t=4)
                 for e in range(2):
                     j = 2 * u + e
                     yt = yts[(g, j)]
@@ -316,5 +297,23 @@ def tile_snnlayer_pa_t_kernel(
                     nc.gpsimd.tensor_scalar(
                         out=yt[:, 0:ns], in0=yt[:, 0:ns], scalar1=-1.0, scalar2=k0[:, j : j + 1], op0=ALU.mult, op1=ALU.add
                     )
-            if not bt_now:
-                quantises(n)
+
+            m = unit_of(n, OFF_MX)
+            if m is not None:
+                g, j = m
+                ns = P * NTS[g]
+                acc = bank("acc", "mx", 2)
+                for ci, c in enumerate(PASS_ORDER):
+                    a_c, a_s = ac[(g, ci // 2)]
+                    lo = (ci % 2) * ns
+                    s0 = (ci * 4 + j) * P
+                    nc.tensor.matmul_mx(
+                        out=acc[:, 0:ns],
+                        lhsT=wcodes[:, s0 : s0 + P].bitcast(FP8X4),
+                        lhsT_scale=wscales[:, s0 : s0 + P],
+                        rhs=a_c[:, lo : lo + ns].bitcast(FP8X4),
+                        rhs_scale=a_s[:, lo : lo + ns],
+                        start=(ci == 0),
+                        stop=(ci == 3),
+                    )
+                mx_at[n] = (g, j, acc)

@@ -21,11 +21,12 @@ PASS_ORDER = (3, 2, 0, 1)
 OFF_Y1 = (0, 2)
 OFF_BT = (1, 3)
 OFF_MEM = (4, 6)
-OFF_QP = (3, 5)
-OFF_MX = 7
-OFF_BK = 12
-N_UNITS = 4 * G + OFF_BK + 4
+OFF_Q = 1
+OFF_MX = 6
+OFF_BK = 11
+N_UNITS = 4 * G + OFF_BK + 5
 PINNED = True
+RUN = 3
 assert sum(NTS) * P == B
 
 
@@ -133,27 +134,26 @@ def tile_snnlayer_pa_t_kernel(
         mx_at = {}
         gws = {}
 
-        def w_quantise(pi):
+        def w_quantise(ci):
             nc.vector.quantize_mx(
-                out=wcodes[:, pi * 1024 : (pi + 1) * 1024].bitcast(FP8X4),
-                scales=wscales[:, pi * 1024 : (pi + 1) * 1024],
-                in_=gws[pi][:],
+                out=wcodes[:, ci * 512 : (ci + 1) * 512].bitcast(FP8X4),
+                scales=wscales[:, ci * 512 : (ci + 1) * 512],
+                in_=gws[ci][:],
             )
 
         load(0, ("ss", "xs", "bs", "ms"))
         load(1, ("ss", "xs", "bs", "ms"))
         for ci, c in enumerate(PASS_ORDER):
-            if ci % 2 == 0:
-                gws[ci // 2] = qp.tile([P, 4096], BF16, name="gw%d" % (ci // 2), tag="gr%d" % (ci // 2), align_bytes=64)
-            gw_f = gws[ci // 2][:].bitcast(F32).rearrange("q (m n u) -> q m n u", m=8, n=P, u=2)
+            gw = qp.tile([P, 2048], BF16, name="gw%d" % c, tag="gr%d" % c, align_bytes=64)
+            gws[ci] = gw
+            gw_f = gw[:].bitcast(F32).rearrange("q (m n u) -> q m n u", m=4, n=P, u=2)
             for jj in range(2):
                 pt = bank("wt", "tx", 4)
                 ptv = pt[:].rearrange("q (m u n) -> q m u n", m=2, u=2, n=P)
                 for m2 in range(2):
                     for u in range(2):
                         nc.tensor.transpose(ptv[:, m2, u, :], w_words(c, 2 * jj + m2, u), ident[:])
-                m0 = 4 * (ci % 2) + 2 * jj
-                dst = gw_f[:, m0 : m0 + 2, :, :]
+                dst = gw_f[:, 2 * jj : 2 * jj + 2, :, :]
                 srcv = ptv.rearrange("q m u n -> q m n u")
                 if jj == 0:
                     nc.scalar.copy(out=dst, in_=srcv)
@@ -161,20 +161,48 @@ def tile_snnlayer_pa_t_kernel(
                     nc.vector.tensor_copy(out=dst, in_=srcv)
             if ci == 0:
                 nc.vector.tensor_mul(out=k0[:], in0=c3[:], in1=bsum[:])
-            if ci == 2:
-                w_quantise(0)
-        w_quantise(1)
+            else:
+                w_quantise(ci - 1)
+        w_quantise(3)
         load(2, ("ss", "xs", "bs", "ms"))
 
         def quantises(n):
-            for g, pi in halves_of(n, OFF_QP):
+            q = unit_of(n, OFF_Q)
+            if q is not None:
+                g, r = q
+                c = PASS_ORDER[r]
                 ns = P * NTS[g]
-                a_c = qp.tile([P, 1024], U32, name="ac%d" % pi, tag="ac%d" % pi, bufs=3, align_bytes=64)
-                a_s = qp.tile([P, 1024], U8, name="as%d" % pi, tag="as%d" % pi, bufs=3, align_bytes=64)
-                nc.vector.quantize_mx(
-                    out=a_c[:, 0 : 2 * ns].bitcast(FP8X4), scales=a_s[:, 0 : 2 * ns], in_=gr[(g, pi)][:, 0 : 8 * ns]
-                )
-                ac[(g, pi)] = (a_c, a_s)
+                a_c = qp.tile([P, 512], U32, name="ac%d" % c, tag="ac%d" % c, bufs=3, align_bytes=64)
+                a_s = qp.tile([P, 512], U8, name="as%d" % c, tag="as%d" % c, bufs=3, align_bytes=64)
+                nc.vector.quantize_mx(out=a_c[:, 0:ns].bitcast(FP8X4), scales=a_s[:, 0:ns], in_=gr[(g, c)][:, 0 : 4 * ns])
+                ac[(g, c)] = (a_c, a_s)
+
+        def mx_pass(k):
+            n, ci = k // 4, k % 4
+            m = unit_of(n, OFF_MX)
+            if m is None:
+                return
+            g, j = m
+            ns = P * NTS[g]
+            if ci == 0:
+                mx_at[n] = (g, j, bank("acc", "mx", 2))
+            acc = mx_at[n][2]
+            a_c, a_s = ac[(g, PASS_ORDER[ci])]
+            s0 = (ci * 4 + j) * P
+            nc.tensor.matmul_mx(
+                out=acc[:, 0:ns],
+                lhsT=wcodes[:, s0 : s0 + P].bitcast(FP8X4),
+                lhsT_scale=wscales[:, s0 : s0 + P],
+                rhs=a_c[:, 0:ns].bitcast(FP8X4),
+                rhs_scale=a_s[:, 0:ns],
+                start=(ci == 0),
+                stop=(ci == 3),
+            )
+
+        def after_step(k):
+            if k % RUN == RUN - 1:
+                for kk in range(k - RUN + 1, k + 1):
+                    mx_pass(kk)
 
         for n in range(N_UNITS):
             if n % 4 == 0 and n > 0:
@@ -182,34 +210,35 @@ def tile_snnlayer_pa_t_kernel(
             elif n % 4 == 3 and n > 3:
                 load(n // 4 + 2, ("bs", "ms"))
 
-            s_copies = []
             a = unit_of(n, 0)
-            if a is not None:
-                g, r = a
-                c = PASS_ORDER[r]
-                nt = NTS[g]
-                tf = min(nt, 2)
-                nf = nt // tf
-                src_t = loaded[(g, "xs" if c < 2 else "ss")]
-                src_f = src_t[:].bitcast(F32)[:, 0 : nt * 512].rearrange("p (t w) -> p t w", t=nt)
-                woff = 256 * (c % 2)
-                if r % 2 == 0:
-                    gr[(g, r // 2)] = qp.tile([P, 4096], BF16, name="gr%d" % (r // 2), tag="gr%d" % (r // 2), align_bytes=64)
-                w0 = (r % 2) * nt * 256
-                gr_f = (
-                    gr[(g, r // 2)][:]
-                    .bitcast(F32)[:, w0 : w0 + nt * 256]
-                    .rearrange("q (h t i u) -> q h t i u", h=nf, t=tf, i=P, u=2)
-                )
-                for h in range(nf):
-                    pt = bank("xt", "tx", 4)
-                    ptv = pt[:, 0 : tf * 256].rearrange("q (t u i) -> q t u i", t=tf, u=2, i=P)
-                    for t2 in range(tf):
-                        for u in range(2):
-                            nc.tensor.transpose(
-                                ptv[:, t2, u, :], src_f[:, tf * h + t2, woff + P * u : woff + P * u + P], ident[:]
-                            )
-                    s_copies.append((gr_f[:, h], ptv.rearrange("q t u i -> q t i u")))
+            for h in range(2):
+                if a is not None:
+                    g, r = a
+                    c = PASS_ORDER[r]
+                    nt = NTS[g]
+                    tf = min(nt, 2)
+                    nf = nt // tf
+                    if h == 0:
+                        gr[(g, c)] = qp.tile([P, 2048], BF16, name="gr%d" % c, tag="gr%d" % c, align_bytes=64)
+                    if h < nf:
+                        src_t = loaded[(g, "xs" if c < 2 else "ss")]
+                        src_f = src_t[:].bitcast(F32)[:, 0 : nt * 512].rearrange("p (t w) -> p t w", t=nt)
+                        woff = 256 * (c % 2)
+                        gr_f = (
+                            gr[(g, c)][:]
+                            .bitcast(F32)[:, 0 : nt * 256]
+                            .rearrange("q (h t i u) -> q h t i u", h=nf, t=tf, i=P, u=2)
+                        )
+                        pt = bank("xt", "tx", 4)
+                        ptv = pt[:, 0 : tf * 256].rearrange("q (t u i) -> q t u i", t=tf, u=2, i=P)
+                        for t2 in range(tf):
+                            for u in range(2):
+                                nc.tensor.transpose(
+                                    ptv[:, t2, u, :], src_f[:, tf * h + t2, woff + P * u : woff + P * u + P], ident[:]
+                                )
+                        nc.scalar.copy(out=gr_f[:, h], in_=ptv.rearrange("q t u i -> q t i u"))
+                after_step(4 * n + h)
+
             bt_now = halves_of(n, OFF_BT)
             mem_now = halves_of(n, OFF_MEM)
             for kind, nm, lst in (("b", "bs", bt_now), ("m", "ms", mem_now)):
@@ -221,38 +250,6 @@ def tile_snnlayer_pa_t_kernel(
                     for t in range(nt):
                         nc.tensor.transpose(pbv[:, t, :], src_f[:, t, P * u : P * u + P], ident[:])
                     tmb[(g, kind, u)] = pb[:].bitcast(BF16)[:, 0 : 2 * nt * P].rearrange("q (s e) -> q s e", e=2)
-            k = unit_of(n, OFF_BK)
-            bk = None
-            if k is not None and k[1] < NTS[k[0]]:
-                g, t = k
-                bk = bank("bk", "tx", 4)
-                bkv = bk[:].rearrange("i (j q) -> i j q", j=4)
-                for j in range(4):
-                    nc.tensor.transpose(bkv[:, j, :], mts[(g, j)][:, t * P : (t + 1) * P], ident[:])
-
-            for dst, srcv in s_copies:
-                nc.scalar.copy(out=dst, in_=srcv)
-            if bk is not None:
-                g, t = k
-                nt = NTS[g]
-                ob = ep.tile([P, R_IN], F32, name="ob", tag="ob", bufs=8)
-                nc.scalar.copy(
-                    out=ob[:].rearrange("i (u q e) -> i u q e", u=2, q=P, e=2),
-                    in_=bk[:].rearrange("i (u e q) -> i u q e", u=2, e=2, q=P),
-                )
-                nc.sync.dma_start(
-                    out=out[base[g] : base[g] + nt * P, :].rearrange("(p t) n -> p t n", t=nt)[:, t, :], in_=ob[:]
-                )
-            for g, u in halves_of(n, OFF_Y1):
-                ns = P * NTS[g]
-                spk4 = gr[(g, 0)][:, 0 : 4 * ns].rearrange("q (s t) -> q s t", t=4)
-                for j in (2 * u, 2 * u + 1):
-                    yt = ep.tile([P, 512], F32, name="yt", tag="yt", bufs=8)
-                    yts[(g, j)] = yt
-                    nc.scalar.activation(
-                        out=yt[:, 0:ns], in_=spk4[:, :, j], func=ACT.Identity, bias=0.1, scale=qq[:, j : j + 1]
-                    )
-
             prev = mx_at.get(n - 1)
             if prev is not None:
                 g, j, acc = prev
@@ -261,7 +258,8 @@ def tile_snnlayer_pa_t_kernel(
                 nc.vector.scalar_tensor_tensor(
                     out=mt[:, 0:ns], in0=acc[:, 0:ns], scalar=c3[:, j : j + 1], in1=mt[:, 0:ns], op0=ALU.mult, op1=ALU.add
                 )
-            quantises(n)
+            if bt_now:
+                quantises(n)
             for g, u in mem_now:
                 ns = P * NTS[g]
                 for e in range(2):
@@ -278,7 +276,7 @@ def tile_snnlayer_pa_t_kernel(
                     )
             for g, u in bt_now:
                 ns = P * NTS[g]
-                spk4 = gr[(g, 0)][:, 0 : 4 * ns].rearrange("q (s t) -> q s t", t=4)
+                spk4 = gr[(g, 3)][:, 0 : 4 * ns].rearrange("q (s t) -> q s t", t=4)
                 for e in range(2):
                     j = 2 * u + e
                     yt = yts[(g, j)]
@@ -297,23 +295,33 @@ def tile_snnlayer_pa_t_kernel(
                     nc.gpsimd.tensor_scalar(
                         out=yt[:, 0:ns], in0=yt[:, 0:ns], scalar1=-1.0, scalar2=k0[:, j : j + 1], op0=ALU.mult, op1=ALU.add
                     )
+            if not bt_now:
+                quantises(n)
+            after_step(4 * n + 2)
 
-            m = unit_of(n, OFF_MX)
-            if m is not None:
-                g, j = m
+            k = unit_of(n, OFF_BK)
+            if k is not None and k[1] < NTS[k[0]]:
+                g, t = k
+                nt = NTS[g]
+                bk = bank("bk", "tx", 4)
+                bkv = bk[:].rearrange("i (j q) -> i j q", j=4)
+                for j in range(4):
+                    nc.tensor.transpose(bkv[:, j, :], mts[(g, j)][:, t * P : (t + 1) * P], ident[:])
+                ob = ep.tile([P, R_IN], F32, name="ob", tag="ob", bufs=8)
+                nc.scalar.copy(
+                    out=ob[:].rearrange("i (u q e) -> i u q e", u=2, q=P, e=2),
+                    in_=bk[:].rearrange("i (u e q) -> i u q e", u=2, e=2, q=P),
+                )
+                nc.sync.dma_start(
+                    out=out[base[g] : base[g] + nt * P, :].rearrange("(p t) n -> p t n", t=nt)[:, t, :], in_=ob[:]
+                )
+            for g, u in halves_of(n, OFF_Y1):
                 ns = P * NTS[g]
-                acc = bank("acc", "mx", 2)
-                for ci, c in enumerate(PASS_ORDER):
-                    a_c, a_s = ac[(g, ci // 2)]
-                    lo = (ci % 2) * ns
-                    s0 = (ci * 4 + j) * P
-                    nc.tensor.matmul_mx(
-                        out=acc[:, 0:ns],
-                        lhsT=wcodes[:, s0 : s0 + P].bitcast(FP8X4),
-                        lhsT_scale=wscales[:, s0 : s0 + P],
-                        rhs=a_c[:, lo : lo + ns].bitcast(FP8X4),
-                        rhs_scale=a_s[:, lo : lo + ns],
-                        start=(ci == 0),
-                        stop=(ci == 3),
+                spk4 = gr[(g, 3)][:, 0 : 4 * ns].rearrange("q (s t) -> q s t", t=4)
+                for j in (2 * u, 2 * u + 1):
+                    yt = ep.tile([P, 512], F32, name="yt", tag="yt", bufs=8)
+                    yts[(g, j)] = yt
+                    nc.scalar.activation(
+                        out=yt[:, 0:ns], in_=spk4[:, :, j], func=ACT.Identity, bias=0.1, scale=qq[:, j : j + 1]
                     )
-                mx_at[n] = (g, j, acc)
+            after_step(4 * n + 3)

@@ -20,13 +20,13 @@ G = len(NTS)
 PASS_ORDER = (3, 2, 0, 1)
 OFF_Y1 = (0, 2)
 OFF_BT = (1, 3)
+OFF_Y4S = (3, 5)
 OFF_MEM = (4, 6)
 OFF_Q = 1
 OFF_MX = 6
 OFF_BK = 11
-N_UNITS = 4 * G + OFF_BK + 5
+N_UNITS = 4 * G + OFF_BK + 4
 PINNED = True
-RUN = 3
 assert sum(NTS) * P == B
 
 
@@ -129,6 +129,7 @@ def tile_snnlayer_pa_t_kernel(
         gr = {}
         ac = {}
         yts = {}
+        ypair = {}
         mts = {}
         tmb = {}
         mx_at = {}
@@ -177,68 +178,35 @@ def tile_snnlayer_pa_t_kernel(
                 nc.vector.quantize_mx(out=a_c[:, 0:ns].bitcast(FP8X4), scales=a_s[:, 0:ns], in_=gr[(g, c)][:, 0 : 4 * ns])
                 ac[(g, c)] = (a_c, a_s)
 
-        def mx_pass(k):
-            n, ci = k // 4, k % 4
-            m = unit_of(n, OFF_MX)
-            if m is None:
-                return
-            g, j = m
-            ns = P * NTS[g]
-            if ci == 0:
-                mx_at[n] = (g, j, bank("acc", "mx", 2))
-            acc = mx_at[n][2]
-            a_c, a_s = ac[(g, PASS_ORDER[ci])]
-            s0 = (ci * 4 + j) * P
-            nc.tensor.matmul_mx(
-                out=acc[:, 0:ns],
-                lhsT=wcodes[:, s0 : s0 + P].bitcast(FP8X4),
-                lhsT_scale=wscales[:, s0 : s0 + P],
-                rhs=a_c[:, 0:ns].bitcast(FP8X4),
-                rhs_scale=a_s[:, 0:ns],
-                start=(ci == 0),
-                stop=(ci == 3),
-            )
-
-        def after_step(k):
-            if k % RUN == RUN - 1:
-                for kk in range(k - RUN + 1, k + 1):
-                    mx_pass(kk)
-
         for n in range(N_UNITS):
             if n % 4 == 0 and n > 0:
                 load(n // 4 + 2, ("ss", "xs"))
             elif n % 4 == 3 and n > 3:
                 load(n // 4 + 2, ("bs", "ms"))
 
+            s_copies = []
             a = unit_of(n, 0)
-            for h in range(2):
-                if a is not None:
-                    g, r = a
-                    c = PASS_ORDER[r]
-                    nt = NTS[g]
-                    tf = min(nt, 2)
-                    nf = nt // tf
-                    if h == 0:
-                        gr[(g, c)] = qp.tile([P, 2048], BF16, name="gr%d" % c, tag="gr%d" % c, align_bytes=64)
-                    if h < nf:
-                        src_t = loaded[(g, "xs" if c < 2 else "ss")]
-                        src_f = src_t[:].bitcast(F32)[:, 0 : nt * 512].rearrange("p (t w) -> p t w", t=nt)
-                        woff = 256 * (c % 2)
-                        gr_f = (
-                            gr[(g, c)][:]
-                            .bitcast(F32)[:, 0 : nt * 256]
-                            .rearrange("q (h t i u) -> q h t i u", h=nf, t=tf, i=P, u=2)
-                        )
-                        pt = bank("xt", "tx", 4)
-                        ptv = pt[:, 0 : tf * 256].rearrange("q (t u i) -> q t u i", t=tf, u=2, i=P)
-                        for t2 in range(tf):
-                            for u in range(2):
-                                nc.tensor.transpose(
-                                    ptv[:, t2, u, :], src_f[:, tf * h + t2, woff + P * u : woff + P * u + P], ident[:]
-                                )
-                        nc.scalar.copy(out=gr_f[:, h], in_=ptv.rearrange("q t u i -> q t i u"))
-                after_step(4 * n + h)
-
+            if a is not None:
+                g, r = a
+                c = PASS_ORDER[r]
+                nt = NTS[g]
+                tf = min(nt, 2)
+                nf = nt // tf
+                src_t = loaded[(g, "xs" if c < 2 else "ss")]
+                src_f = src_t[:].bitcast(F32)[:, 0 : nt * 512].rearrange("p (t w) -> p t w", t=nt)
+                woff = 256 * (c % 2)
+                grt = qp.tile([P, 2048], BF16, name="gr%d" % c, tag="gr%d" % c, align_bytes=64)
+                gr[(g, c)] = grt
+                gr_f = grt[:].bitcast(F32)[:, 0 : nt * 256].rearrange("q (h t i u) -> q h t i u", h=nf, t=tf, i=P, u=2)
+                for h in range(nf):
+                    pt = bank("xt", "tx", 4)
+                    ptv = pt[:, 0 : tf * 256].rearrange("q (t u i) -> q t u i", t=tf, u=2, i=P)
+                    for t2 in range(tf):
+                        for u in range(2):
+                            nc.tensor.transpose(
+                                ptv[:, t2, u, :], src_f[:, tf * h + t2, woff + P * u : woff + P * u + P], ident[:]
+                            )
+                    s_copies.append((gr_f[:, h], ptv.rearrange("q t u i -> q t i u")))
             bt_now = halves_of(n, OFF_BT)
             mem_now = halves_of(n, OFF_MEM)
             for kind, nm, lst in (("b", "bs", bt_now), ("m", "ms", mem_now)):
@@ -250,6 +218,46 @@ def tile_snnlayer_pa_t_kernel(
                     for t in range(nt):
                         nc.tensor.transpose(pbv[:, t, :], src_f[:, t, P * u : P * u + P], ident[:])
                     tmb[(g, kind, u)] = pb[:].bitcast(BF16)[:, 0 : 2 * nt * P].rearrange("q (s e) -> q s e", e=2)
+            k = unit_of(n, OFF_BK)
+            bk = None
+            if k is not None and k[1] < NTS[k[0]]:
+                g, t = k
+                bk = bank("bk", "tx", 4)
+                bkv = bk[:].rearrange("i (j q) -> i j q", j=4)
+                for j in range(4):
+                    nc.tensor.transpose(bkv[:, j, :], mts[(g, j)][:, t * P : (t + 1) * P], ident[:])
+
+            for dst, srcv in s_copies:
+                nc.scalar.copy(out=dst, in_=srcv)
+            for g, u in halves_of(n, OFF_Y4S):
+                ns = P * NTS[g]
+                j = 2 * u + 1
+                nc.scalar.activation(
+                    out=yts[(g, j)], in_=yts[(g, j)], func=ACT.Identity, bias=k0[:, j : j + 1], scale=-1.0
+                )
+            if bk is not None:
+                g, t = k
+                nt = NTS[g]
+                ob = ep.tile([P, R_IN], F32, name="ob", tag="ob", bufs=8)
+                nc.scalar.copy(
+                    out=ob[:].rearrange("i (u q e) -> i u q e", u=2, q=P, e=2),
+                    in_=bk[:].rearrange("i (u e q) -> i u q e", u=2, e=2, q=P),
+                )
+                nc.sync.dma_start(
+                    out=out[base[g] : base[g] + nt * P, :].rearrange("(p t) n -> p t n", t=nt)[:, t, :], in_=ob[:]
+                )
+            for g, u in halves_of(n, OFF_Y1):
+                ns = P * NTS[g]
+                spk4 = gr[(g, 3)][:, 0 : 4 * ns].rearrange("q (s t) -> q s t", t=4)
+                ytp = ep.tile([P, 1024], F32, name="ytp", tag="yt", bufs=4)
+                ypair[(g, u)] = ytp[:, 0 : 2 * ns].rearrange("q (e s) -> q e s", e=2)
+                for e in range(2):
+                    j = 2 * u + e
+                    yts[(g, j)] = ytp[:, e * ns : (e + 1) * ns]
+                    nc.scalar.activation(
+                        out=yts[(g, j)], in_=spk4[:, :, j], func=ACT.Identity, bias=0.1, scale=qq[:, j : j + 1]
+                    )
+
             prev = mx_at.get(n - 1)
             if prev is not None:
                 g, j, acc = prev
@@ -270,7 +278,7 @@ def tile_snnlayer_pa_t_kernel(
                         out=mt[:, 0:ns],
                         in0=tmb[(g, "m", u)][:, :, e],
                         scalar=aa[:, j : j + 1],
-                        in1=yts[(g, j)][:, 0:ns],
+                        in1=yts[(g, j)],
                         op0=ALU.mult,
                         op1=ALU.add,
                     )
@@ -279,49 +287,42 @@ def tile_snnlayer_pa_t_kernel(
                 spk4 = gr[(g, 3)][:, 0 : 4 * ns].rearrange("q (s t) -> q s t", t=4)
                 for e in range(2):
                     j = 2 * u + e
-                    yt = yts[(g, j)]
                     nc.vector.scalar_tensor_tensor(
-                        out=yt[:, 0:ns],
+                        out=yts[(g, j)],
                         in0=tmb[(g, "b", u)][:, :, e],
                         scalar=pq[:, j : j + 1],
-                        in1=yt[:, 0:ns],
+                        in1=yts[(g, j)],
                         op0=ALU.mult,
                         op1=ALU.add,
                     )
-                for e in range(2):
-                    j = 2 * u + e
-                    yt = yts[(g, j)]
-                    nc.gpsimd.tensor_tensor(out=yt[:, 0:ns], in0=yt[:, 0:ns], in1=spk4[:, :, j], op=ALU.mult)
-                    nc.gpsimd.tensor_scalar(
-                        out=yt[:, 0:ns], in0=yt[:, 0:ns], scalar1=-1.0, scalar2=k0[:, j : j + 1], op0=ALU.mult, op1=ALU.add
-                    )
+                nc.gpsimd.tensor_tensor(
+                    out=ypair[(g, u)],
+                    in0=ypair[(g, u)],
+                    in1=spk4.rearrange("q s t -> q t s")[:, 2 * u : 2 * u + 2, :],
+                    op=ALU.mult,
+                )
+                j = 2 * u
+                nc.gpsimd.tensor_scalar(
+                    out=yts[(g, j)], in0=yts[(g, j)], scalar1=-1.0, scalar2=k0[:, j : j + 1], op0=ALU.mult, op1=ALU.add
+                )
             if not bt_now:
                 quantises(n)
-            after_step(4 * n + 2)
 
-            k = unit_of(n, OFF_BK)
-            if k is not None and k[1] < NTS[k[0]]:
-                g, t = k
-                nt = NTS[g]
-                bk = bank("bk", "tx", 4)
-                bkv = bk[:].rearrange("i (j q) -> i j q", j=4)
-                for j in range(4):
-                    nc.tensor.transpose(bkv[:, j, :], mts[(g, j)][:, t * P : (t + 1) * P], ident[:])
-                ob = ep.tile([P, R_IN], F32, name="ob", tag="ob", bufs=8)
-                nc.scalar.copy(
-                    out=ob[:].rearrange("i (u q e) -> i u q e", u=2, q=P, e=2),
-                    in_=bk[:].rearrange("i (u e q) -> i u q e", u=2, e=2, q=P),
-                )
-                nc.sync.dma_start(
-                    out=out[base[g] : base[g] + nt * P, :].rearrange("(p t) n -> p t n", t=nt)[:, t, :], in_=ob[:]
-                )
-            for g, u in halves_of(n, OFF_Y1):
+            m = unit_of(n, OFF_MX)
+            if m is not None:
+                g, j = m
                 ns = P * NTS[g]
-                spk4 = gr[(g, 3)][:, 0 : 4 * ns].rearrange("q (s t) -> q s t", t=4)
-                for j in (2 * u, 2 * u + 1):
-                    yt = ep.tile([P, 512], F32, name="yt", tag="yt", bufs=8)
-                    yts[(g, j)] = yt
-                    nc.scalar.activation(
-                        out=yt[:, 0:ns], in_=spk4[:, :, j], func=ACT.Identity, bias=0.1, scale=qq[:, j : j + 1]
+                acc = bank("acc", "mx", 2)
+                for ci, c in enumerate(PASS_ORDER):
+                    a_c, a_s = ac[(g, c)]
+                    s0 = (ci * 4 + j) * P
+                    nc.tensor.matmul_mx(
+                        out=acc[:, 0:ns],
+                        lhsT=wcodes[:, s0 : s0 + P].bitcast(FP8X4),
+                        lhsT_scale=wscales[:, s0 : s0 + P],
+                        rhs=a_c[:, 0:ns].bitcast(FP8X4),
+                        rhs_scale=a_s[:, 0:ns],
+                        start=(ci == 0),
+                        stop=(ci == 3),
                     )
-            after_step(4 * n + 3)
+                mx_at[n] = (g, j, acc)

@@ -15,18 +15,18 @@ P = 128
 B, IN_DIM, R_IN = 4096, 1024, 512
 FLOPS = 2 * B * (IN_DIM + 2 * R_IN) * R_IN
 
-NTS = (1, 1, 2, 4, 4, 4, 4, 4, 4, 2, 1, 1)
+NTS = (4, 4, 4, 4, 4, 4, 4, 4)
 G = len(NTS)
 PASS_ORDER = (3, 2, 0, 1)
 OFF_Y1 = (0, 2)
 OFF_BT = (1, 3)
-OFF_Y4S = (3, 5)
 OFF_MEM = (4, 6)
 OFF_Q = 1
 OFF_MX = 6
 OFF_BK = 11
 N_UNITS = 4 * G + OFF_BK + 4
 PINNED = True
+SPLIT_GROUPS = 2
 assert sum(NTS) * P == B
 
 
@@ -73,46 +73,53 @@ def tile_snnlayer_pa_t_kernel(
             for nm in names:
                 src, width = srcs[nm]
                 dst = ld.tile([P, 4 * width], BF16, name=nm, tag=nm)
-                nc.sync.dma_start(
-                    out=dst[:, 0 : nt * width].rearrange("p (t k) -> p t k", t=nt),
-                    in_=src[base[g] : base[g] + nt * P, :].rearrange("(p t) k -> p t k", t=nt),
-                )
+                dst_v = dst[:, 0 : nt * width].rearrange("p (t k) -> p t k", t=nt)
+                src_v = src[base[g] : base[g] + nt * P, :].rearrange("(p t) k -> p t k", t=nt)
+                if g < SPLIT_GROUPS:
+                    for h in range(2):
+                        nc.sync.dma_start(out=dst_v[:, 2 * h : 2 * h + 2, :], in_=src_v[:, 2 * h : 2 * h + 2, :])
+                else:
+                    nc.sync.dma_start(out=dst_v, in_=src_v)
                 loaded[(g, nm)] = dst
 
         craw = const.tile([P, 256], BF16, name="craw")
         nc.vector.memset(craw[:], 0.0)
-        for v, vec in enumerate((b_x2in, b_rec4in, b_out2in, tau_adp_in, tau_m_in)):
-            nc.sync.dma_start(out=craw[2 * v : 2 * v + 2, :], in_=vec.rearrange("(u w) -> u w", u=2))
         ident = const.tile([P, P], F32, name="ident")
         make_identity(nc, ident[:])
 
         wro = ld.tile([P, 4096], BF16, name="wro", tag="ss")
         wx = ld.tile([P, 4096], BF16, name="wx", tag="xs")
-        for dst, src in ((wro[:, 0:2048], W_rec4in), (wro[:, 2048:4096], W_out2in), (wx[:], W_x2in)):
-            nc.sync.dma_start(
-                out=dst.rearrange("p (u e k) -> p u e k", u=2, e=2),
-                in_=src.rearrange("(u p e) k -> p u e k", u=2, p=P, e=2),
-            )
+        for wi, (dst, src) in enumerate(((wro[:, 0:2048], W_rec4in), (wro[:, 2048:4096], W_out2in), (wx[:], W_x2in))):
+            dst_v = dst.rearrange("p (u e k) -> p u e k", u=2, e=2)
+            src_v = src.rearrange("(u p e) k -> p u e k", u=2, p=P, e=2)
+            for u in range(2):
+                nc.sync.dma_start(out=dst_v[:, u], in_=src_v[:, u])
+            if wi == 0:
+                for v, vec in enumerate((b_x2in, b_rec4in, b_out2in, tau_adp_in, tau_m_in)):
+                    nc.sync.dma_start(out=craw[2 * v : 2 * v + 2, :], in_=vec.rearrange("(u w) -> u w", u=2))
 
-        cps = bank("cps", "tx", 4)
-        nc.tensor.transpose(cps[:, 0:P], craw[:].bitcast(F32), ident[:])
         cst = const.tile([P, 20], F32, name="cst")
-        nc.vector.tensor_copy(out=cst[:], in_=cps[:].bitcast(BF16)[:, 0:20])
         bsum = const.tile([P, 4], F32, name="bsum")
-        nc.vector.tensor_add(out=bsum[:], in0=cst[:, 0:4], in1=cst[:, 4:8])
-        nc.vector.tensor_add(out=bsum[:], in0=bsum[:], in1=cst[:, 8:12])
         sg = const.tile([P, 8], F32, name="sg")
         ng = const.tile([P, 8], F32, name="ng")
-        nc.scalar.activation(out=sg[:], in_=cst[:, 12:20], func=ACT.Sigmoid)
-        nc.scalar.activation(out=ng[:], in_=cst[:, 12:20], func=ACT.Sigmoid, scale=-1.0)
         pq = const.tile([P, 4], F32, name="pq")
         qq = const.tile([P, 4], F32, name="qq")
         c3 = const.tile([P, 4], F32, name="c3")
         k0 = const.tile([P, 4], F32, name="k0")
-        nc.scalar.mul(out=qq[:], in_=ng[:, 0:4], mul=1.8)
-        nc.scalar.mul(out=pq[:], in_=sg[:, 0:4], mul=1.8)
-        nc.scalar.mul(out=c3[:], in_=ng[:, 4:8], mul=3.0)
         aa = sg[:, 4:8]
+
+        def make_constants():
+            cps = bank("cps", "tx", 4)
+            nc.tensor.transpose(cps[:, 0:P], craw[:].bitcast(F32), ident[:])
+            nc.vector.tensor_copy(out=cst[:], in_=cps[:].bitcast(BF16)[:, 0:20])
+            nc.vector.tensor_add(out=bsum[:], in0=cst[:, 0:4], in1=cst[:, 4:8])
+            nc.vector.tensor_add(out=bsum[:], in0=bsum[:], in1=cst[:, 8:12])
+            nc.scalar.activation(out=sg[:], in_=cst[:, 12:20], func=ACT.Sigmoid)
+            nc.scalar.activation(out=ng[:], in_=cst[:, 12:20], func=ACT.Sigmoid, scale=-1.0)
+            nc.scalar.mul(out=qq[:], in_=ng[:, 0:4], mul=1.8)
+            nc.scalar.mul(out=pq[:], in_=sg[:, 0:4], mul=1.8)
+            nc.scalar.mul(out=c3[:], in_=ng[:, 4:8], mul=3.0)
+            nc.vector.tensor_mul(out=k0[:], in0=c3[:], in1=bsum[:])
 
         wcodes = const.tile([P, 16 * P], U32, name="wcodes", align_bytes=64)
         wscales = const.tile([P, 16 * P], U8, name="wscales", align_bytes=64)
@@ -129,7 +136,6 @@ def tile_snnlayer_pa_t_kernel(
         gr = {}
         ac = {}
         yts = {}
-        ypair = {}
         mts = {}
         tmb = {}
         mx_at = {}
@@ -161,7 +167,7 @@ def tile_snnlayer_pa_t_kernel(
                 else:
                     nc.vector.tensor_copy(out=dst, in_=srcv)
             if ci == 0:
-                nc.vector.tensor_mul(out=k0[:], in0=c3[:], in1=bsum[:])
+                make_constants()
             else:
                 w_quantise(ci - 1)
         w_quantise(3)
@@ -229,12 +235,6 @@ def tile_snnlayer_pa_t_kernel(
 
             for dst, srcv in s_copies:
                 nc.scalar.copy(out=dst, in_=srcv)
-            for g, u in halves_of(n, OFF_Y4S):
-                ns = P * NTS[g]
-                j = 2 * u + 1
-                nc.scalar.activation(
-                    out=yts[(g, j)], in_=yts[(g, j)], func=ACT.Identity, bias=k0[:, j : j + 1], scale=-1.0
-                )
             if bk is not None:
                 g, t = k
                 nt = NTS[g]
@@ -249,13 +249,11 @@ def tile_snnlayer_pa_t_kernel(
             for g, u in halves_of(n, OFF_Y1):
                 ns = P * NTS[g]
                 spk4 = gr[(g, 3)][:, 0 : 4 * ns].rearrange("q (s t) -> q s t", t=4)
-                ytp = ep.tile([P, 1024], F32, name="ytp", tag="yt", bufs=4)
-                ypair[(g, u)] = ytp[:, 0 : 2 * ns].rearrange("q (e s) -> q e s", e=2)
-                for e in range(2):
-                    j = 2 * u + e
-                    yts[(g, j)] = ytp[:, e * ns : (e + 1) * ns]
+                for j in (2 * u, 2 * u + 1):
+                    yt = ep.tile([P, 512], F32, name="yt", tag="yt", bufs=8)
+                    yts[(g, j)] = yt
                     nc.scalar.activation(
-                        out=yts[(g, j)], in_=spk4[:, :, j], func=ACT.Identity, bias=0.1, scale=qq[:, j : j + 1]
+                        out=yt[:, 0:ns], in_=spk4[:, :, j], func=ACT.Identity, bias=0.1, scale=qq[:, j : j + 1]
                     )
 
             prev = mx_at.get(n - 1)
@@ -278,7 +276,7 @@ def tile_snnlayer_pa_t_kernel(
                         out=mt[:, 0:ns],
                         in0=tmb[(g, "m", u)][:, :, e],
                         scalar=aa[:, j : j + 1],
-                        in1=yts[(g, j)],
+                        in1=yts[(g, j)][:, 0:ns],
                         op0=ALU.mult,
                         op1=ALU.add,
                     )
@@ -287,24 +285,22 @@ def tile_snnlayer_pa_t_kernel(
                 spk4 = gr[(g, 3)][:, 0 : 4 * ns].rearrange("q (s t) -> q s t", t=4)
                 for e in range(2):
                     j = 2 * u + e
+                    yt = yts[(g, j)]
                     nc.vector.scalar_tensor_tensor(
-                        out=yts[(g, j)],
+                        out=yt[:, 0:ns],
                         in0=tmb[(g, "b", u)][:, :, e],
                         scalar=pq[:, j : j + 1],
-                        in1=yts[(g, j)],
+                        in1=yt[:, 0:ns],
                         op0=ALU.mult,
                         op1=ALU.add,
                     )
-                nc.gpsimd.tensor_tensor(
-                    out=ypair[(g, u)],
-                    in0=ypair[(g, u)],
-                    in1=spk4.rearrange("q s t -> q t s")[:, 2 * u : 2 * u + 2, :],
-                    op=ALU.mult,
-                )
-                j = 2 * u
-                nc.gpsimd.tensor_scalar(
-                    out=yts[(g, j)], in0=yts[(g, j)], scalar1=-1.0, scalar2=k0[:, j : j + 1], op0=ALU.mult, op1=ALU.add
-                )
+                for e in range(2):
+                    j = 2 * u + e
+                    yt = yts[(g, j)]
+                    nc.gpsimd.tensor_tensor(out=yt[:, 0:ns], in0=yt[:, 0:ns], in1=spk4[:, :, j], op=ALU.mult)
+                    nc.gpsimd.tensor_scalar(
+                        out=yt[:, 0:ns], in0=yt[:, 0:ns], scalar1=-1.0, scalar2=k0[:, j : j + 1], op0=ALU.mult, op1=ALU.add
+                    )
             if not bt_now:
                 quantises(n)
 

@@ -19,8 +19,9 @@ NTS = (4, 4, 4, 4, 4, 4, 4, 4)
 G = len(NTS)
 PASS_ORDER = (3, 2, 0, 1)
 OFF_Y1 = (0, 2)
-OFF_BT = (1, 3)
-OFF_MEM = (4, 6)
+OFF_MEM = (1, 3)
+OFF_BT = (4, 6)
+OFF_BS = (1, 3)
 OFF_Q = 1
 OFF_MX = 6
 OFF_BK = 11
@@ -102,8 +103,8 @@ def tile_snnlayer_pa_t_kernel(
         bsum = const.tile([P, 4], F32, name="bsum")
         sg = const.tile([P, 8], F32, name="sg")
         ng = const.tile([P, 8], F32, name="ng")
-        pq = const.tile([P, 4], F32, name="pq")
-        qq = const.tile([P, 4], F32, name="qq")
+        md = const.tile([P, 4], F32, name="md")
+        mc = const.tile([P, 4], F32, name="mc")
         c3 = const.tile([P, 4], F32, name="c3")
         k0 = const.tile([P, 4], F32, name="k0")
         aa = sg[:, 4:8]
@@ -116,8 +117,8 @@ def tile_snnlayer_pa_t_kernel(
             nc.vector.tensor_add(out=bsum[:], in0=bsum[:], in1=cst[:, 8:12])
             nc.scalar.activation(out=sg[:], in_=cst[:, 12:20], func=ACT.Sigmoid)
             nc.scalar.activation(out=ng[:], in_=cst[:, 12:20], func=ACT.Sigmoid, scale=-1.0)
-            nc.scalar.mul(out=qq[:], in_=ng[:, 0:4], mul=1.8)
-            nc.scalar.mul(out=pq[:], in_=sg[:, 0:4], mul=1.8)
+            nc.vector.tensor_scalar(out=mc[:], in0=ng[:, 0:4], scalar1=-1.8, scalar2=-0.1, op0=ALU.mult, op1=ALU.add)
+            nc.scalar.mul(out=md[:], in_=sg[:, 0:4], mul=-1.8)
             nc.scalar.mul(out=c3[:], in_=ng[:, 4:8], mul=3.0)
             nc.vector.tensor_mul(out=k0[:], in0=c3[:], in1=bsum[:])
 
@@ -148,8 +149,8 @@ def tile_snnlayer_pa_t_kernel(
                 in_=gws[ci][:],
             )
 
-        load(0, ("ss", "xs", "bs", "ms"))
-        load(1, ("ss", "xs", "bs", "ms"))
+        load(0, ("ss", "ms", "xs", "bs"))
+        load(1, ("ss", "ms", "xs", "bs"))
         for ci, c in enumerate(PASS_ORDER):
             gw = qp.tile([P, 2048], BF16, name="gw%d" % c, tag="gr%d" % c, align_bytes=64)
             gws[ci] = gw
@@ -171,7 +172,7 @@ def tile_snnlayer_pa_t_kernel(
             else:
                 w_quantise(ci - 1)
         w_quantise(3)
-        load(2, ("ss", "xs", "bs", "ms"))
+        load(2, ("ss", "ms", "xs", "bs"))
 
         def quantises(n):
             q = unit_of(n, OFF_Q)
@@ -188,7 +189,7 @@ def tile_snnlayer_pa_t_kernel(
             if n % 4 == 0 and n > 0:
                 load(n // 4 + 2, ("ss", "xs"))
             elif n % 4 == 3 and n > 3:
-                load(n // 4 + 2, ("bs", "ms"))
+                load(n // 4 + 2, ("ms", "bs"))
 
             s_copies = []
             a = unit_of(n, 0)
@@ -215,7 +216,7 @@ def tile_snnlayer_pa_t_kernel(
                     s_copies.append((gr_f[:, h], ptv.rearrange("q t u i -> q t i u")))
             bt_now = halves_of(n, OFF_BT)
             mem_now = halves_of(n, OFF_MEM)
-            for kind, nm, lst in (("b", "bs", bt_now), ("m", "ms", mem_now)):
+            for kind, nm, lst in (("m", "ms", mem_now), ("b", "bs", bt_now)):
                 for g, u in lst:
                     nt = NTS[g]
                     src_f = loaded[(g, nm)][:].bitcast(F32)[:, 0 : nt * 256].rearrange("p (t w) -> p t w", t=nt)
@@ -253,7 +254,7 @@ def tile_snnlayer_pa_t_kernel(
                     yt = ep.tile([P, 512], F32, name="yt", tag="yt", bufs=8)
                     yts[(g, j)] = yt
                     nc.scalar.activation(
-                        out=yt[:, 0:ns], in_=spk4[:, :, j], func=ACT.Identity, bias=0.1, scale=qq[:, j : j + 1]
+                        out=yt[:, 0:ns], in_=spk4[:, :, j], func=ACT.Identity, bias=k0[:, j : j + 1], scale=mc[:, j : j + 1]
                     )
 
             prev = mx_at.get(n - 1)
@@ -264,9 +265,9 @@ def tile_snnlayer_pa_t_kernel(
                 nc.vector.scalar_tensor_tensor(
                     out=mt[:, 0:ns], in0=acc[:, 0:ns], scalar=c3[:, j : j + 1], in1=mt[:, 0:ns], op0=ALU.mult, op1=ALU.add
                 )
-            if bt_now:
+            if mem_now:
                 quantises(n)
-            for g, u in mem_now:
+            for g, u in bt_now:
                 ns = P * NTS[g]
                 for e in range(2):
                     j = 2 * u + e
@@ -274,34 +275,31 @@ def tile_snnlayer_pa_t_kernel(
                     mts[(g, j)] = mt
                     nc.vector.scalar_tensor_tensor(
                         out=mt[:, 0:ns],
-                        in0=tmb[(g, "m", u)][:, :, e],
-                        scalar=aa[:, j : j + 1],
+                        in0=tmb[(g, "b", u)][:, :, e],
+                        scalar=md[:, j : j + 1],
                         in1=yts[(g, j)][:, 0:ns],
                         op0=ALU.mult,
                         op1=ALU.add,
                     )
-            for g, u in bt_now:
+            for g, u in halves_of(n, OFF_BS):
+                nt = NTS[g]
+                bv = loaded[(g, "bs")][:, 0 : nt * 512].rearrange("p (t k) -> p t k", t=nt)[:, :, 256 * u : 256 * u + 256]
+                sv = loaded[(g, "ss")][:, 0 : nt * 1024].rearrange("p (t k) -> p t k", t=nt)[:, :, 512 + 256 * u : 768 + 256 * u]
+                nc.vector.tensor_tensor(out=bv, in0=bv, in1=sv, op=ALU.mult)
+            for g, u in mem_now:
                 ns = P * NTS[g]
-                spk4 = gr[(g, 3)][:, 0 : 4 * ns].rearrange("q (s t) -> q s t", t=4)
                 for e in range(2):
                     j = 2 * u + e
                     yt = yts[(g, j)]
                     nc.vector.scalar_tensor_tensor(
                         out=yt[:, 0:ns],
-                        in0=tmb[(g, "b", u)][:, :, e],
-                        scalar=pq[:, j : j + 1],
+                        in0=tmb[(g, "m", u)][:, :, e],
+                        scalar=aa[:, j : j + 1],
                         in1=yt[:, 0:ns],
                         op0=ALU.mult,
                         op1=ALU.add,
                     )
-                for e in range(2):
-                    j = 2 * u + e
-                    yt = yts[(g, j)]
-                    nc.gpsimd.tensor_tensor(out=yt[:, 0:ns], in0=yt[:, 0:ns], in1=spk4[:, :, j], op=ALU.mult)
-                    nc.gpsimd.tensor_scalar(
-                        out=yt[:, 0:ns], in0=yt[:, 0:ns], scalar1=-1.0, scalar2=k0[:, j : j + 1], op0=ALU.mult, op1=ALU.add
-                    )
-            if not bt_now:
+            if not mem_now:
                 quantises(n)
 
             m = unit_of(n, OFF_MX)

@@ -216,10 +216,10 @@ def tile_snnlayer_pa_t_kernel(
                     s_copies.append((gr_f[:, h], ptv.rearrange("q t u i -> q t i u")))
             bt_now = halves_of(n, OFF_BT)
             mem_now = halves_of(n, OFF_MEM)
-            for kind, nm, lst in (("m", "ms", mem_now), ("b", "bs", bt_now)):
+            for kind, lst in (("m", mem_now), ("b", bt_now)):
                 for g, u in lst:
                     nt = NTS[g]
-                    src_f = loaded[(g, nm)][:].bitcast(F32)[:, 0 : nt * 256].rearrange("p (t w) -> p t w", t=nt)
+                    src_f = loaded[(g, "ms")][:].bitcast(F32)[:, 0 : nt * 256].rearrange("p (t w) -> p t w", t=nt)
                     pb = bank("p" + kind, "tm", 2)
                     pbv = pb[:, 0 : nt * P].rearrange("q (t i) -> q t i", t=nt)
                     for t in range(nt):
@@ -285,7 +285,9 @@ def tile_snnlayer_pa_t_kernel(
                 nt = NTS[g]
                 bv = loaded[(g, "bs")][:, 0 : nt * 512].rearrange("p (t k) -> p t k", t=nt)[:, :, 256 * u : 256 * u + 256]
                 sv = loaded[(g, "ss")][:, 0 : nt * 1024].rearrange("p (t k) -> p t k", t=nt)[:, :, 512 + 256 * u : 768 + 256 * u]
-                nc.vector.tensor_tensor(out=bv, in0=bv, in1=sv, op=ALU.mult)
+                pv = loaded[(g, "ms")][:, 0 : nt * 512].rearrange("p (t k) -> p t k", t=nt)[:, :, 256 * u : 256 * u + 256]
+                for t in range(nt):
+                    nc.gpsimd.tensor_tensor(out=pv[:, t, :], in0=bv[:, t, :], in1=sv[:, t, :], op=ALU.mult)
             for g, u in mem_now:
                 ns = P * NTS[g]
                 for e in range(2):

@@ -18,13 +18,15 @@ FLOPS = 2 * B * (IN_DIM + 2 * R_IN) * R_IN
 NTS = (4, 4, 4, 4, 4, 4, 4, 4)
 G = len(NTS)
 PASS_ORDER = (3, 2, 0, 1)
-OFF_Y1 = (0, 2)
-OFF_MEM = (1, 3)
-OFF_BT = (4, 6)
-OFF_BS = (1, 3)
+OFF_BT = (1, 3)
+OFF_V = 1
+OFF_Z = 2
+OFF_Z2 = 3
 OFF_Q = 1
-OFF_MX = 6
-OFF_BK = 11
+OFF_MX = 5
+OFF_BK = 10
+MN_LEAD = 3
+VT_BUFS = 8
 N_UNITS = 4 * G + OFF_BK + 4
 PINNED = True
 SPLIT_GROUPS = 2
@@ -110,7 +112,7 @@ def tile_snnlayer_pa_t_kernel(
         aa = sg[:, 4:8]
 
         def make_constants():
-            cps = bank("cps", "tx", 4)
+            cps = bank("cps", "tx", 3)
             nc.tensor.transpose(cps[:, 0:P], craw[:].bitcast(F32), ident[:])
             nc.vector.tensor_copy(out=cst[:], in_=cps[:].bitcast(BF16)[:, 0:20])
             nc.vector.tensor_add(out=bsum[:], in0=cst[:, 0:4], in1=cst[:, 4:8])
@@ -121,6 +123,17 @@ def tile_snnlayer_pa_t_kernel(
             nc.scalar.mul(out=md[:], in_=sg[:, 0:4], mul=-1.8)
             nc.scalar.mul(out=c3[:], in_=ng[:, 4:8], mul=3.0)
             nc.vector.tensor_mul(out=k0[:], in0=c3[:], in1=bsum[:])
+
+        a_nat = const.tile([P, R_IN], F32, name="a_nat")
+
+        def make_a_nat():
+            aps = bank("aps", "tx", 3)
+            for j in range(4):
+                nc.tensor.transpose(aps[:, j * P : (j + 1) * P], aa[:, j : j + 1].to_broadcast([P, P]), ident[:])
+            nc.scalar.copy(
+                out=a_nat[:].rearrange("i (u q e) -> i u q e", u=2, q=P, e=2),
+                in_=aps[:].rearrange("i (u e q) -> i u q e", u=2, e=2, q=P),
+            )
 
         wcodes = const.tile([P, 16 * P], U32, name="wcodes", align_bytes=64)
         wscales = const.tile([P, 16 * P], U8, name="wscales", align_bytes=64)
@@ -136,11 +149,23 @@ def tile_snnlayer_pa_t_kernel(
 
         gr = {}
         ac = {}
-        yts = {}
+        vts = {}
         mts = {}
         tmb = {}
         mx_at = {}
+        bk_at = {}
+        mns = {}
         gws = {}
+
+        def make_mn(i, grt):
+            if grt is None:
+                mn = ep.tile([P, R_IN], F32, name="mn", tag="mn", bufs=4)
+                mn = mn[:]
+            else:
+                mn = grt[:]
+            mns[i] = mn
+            mv = loaded[(i // 4, "ms")][:].rearrange("p (t k) -> p t k", t=4)
+            nc.gpsimd.tensor_tensor(out=mn, in0=mv[:, i % 4, :], in1=a_nat[:], op=ALU.mult)
 
         def w_quantise(ci):
             nc.vector.quantize_mx(
@@ -149,14 +174,15 @@ def tile_snnlayer_pa_t_kernel(
                 in_=gws[ci][:],
             )
 
-        load(0, ("ss", "ms", "xs", "bs"))
-        load(1, ("ss", "ms", "xs", "bs"))
+        load(0, ("ss", "xs", "bs"))
+        load(1, ("ss", "xs", "bs"))
+        load(0, ("ms",))
         for ci, c in enumerate(PASS_ORDER):
             gw = qp.tile([P, 2048], BF16, name="gw%d" % c, tag="gr%d" % c, align_bytes=64)
             gws[ci] = gw
             gw_f = gw[:].bitcast(F32).rearrange("q (m n u) -> q m n u", m=4, n=P, u=2)
             for jj in range(2):
-                pt = bank("wt", "tx", 4)
+                pt = bank("wt", "tx", 3)
                 ptv = pt[:].rearrange("q (m u n) -> q m u n", m=2, u=2, n=P)
                 for m2 in range(2):
                     for u in range(2):
@@ -172,7 +198,9 @@ def tile_snnlayer_pa_t_kernel(
             else:
                 w_quantise(ci - 1)
         w_quantise(3)
-        load(2, ("ss", "ms", "xs", "bs"))
+        make_a_nat()
+        load(2, ("ss", "xs", "bs"))
+        load(1, ("ms",))
 
         def quantises(n):
             q = unit_of(n, OFF_Q)
@@ -189,7 +217,9 @@ def tile_snnlayer_pa_t_kernel(
             if n % 4 == 0 and n > 0:
                 load(n // 4 + 2, ("ss", "xs"))
             elif n % 4 == 3 and n > 3:
-                load(n // 4 + 2, ("ms", "bs"))
+                load(n // 4 + 2, ("bs",))
+            if n % 4 == 1 and n // 4 >= 2:
+                load(n // 4, ("ms",))
 
             s_copies = []
             a = unit_of(n, 0)
@@ -206,7 +236,7 @@ def tile_snnlayer_pa_t_kernel(
                 gr[(g, c)] = grt
                 gr_f = grt[:].bitcast(F32)[:, 0 : nt * 256].rearrange("q (h t i u) -> q h t i u", h=nf, t=tf, i=P, u=2)
                 for h in range(nf):
-                    pt = bank("xt", "tx", 4)
+                    pt = bank("xt", "tx", 3)
                     ptv = pt[:, 0 : tf * 256].rearrange("q (t u i) -> q t u i", t=tf, u=2, i=P)
                     for t2 in range(tf):
                         for u in range(2):
@@ -214,49 +244,68 @@ def tile_snnlayer_pa_t_kernel(
                                 ptv[:, t2, u, :], src_f[:, tf * h + t2, woff + P * u : woff + P * u + P], ident[:]
                             )
                     s_copies.append((gr_f[:, h], ptv.rearrange("q t u i -> q t i u")))
-            bt_now = halves_of(n, OFF_BT)
-            mem_now = halves_of(n, OFF_MEM)
-            for kind, lst in (("m", mem_now), ("b", bt_now)):
-                for g, u in lst:
-                    nt = NTS[g]
-                    src_f = loaded[(g, "ms")][:].bitcast(F32)[:, 0 : nt * 256].rearrange("p (t w) -> p t w", t=nt)
-                    pb = bank("p" + kind, "tm", 2)
-                    pbv = pb[:, 0 : nt * P].rearrange("q (t i) -> q t i", t=nt)
-                    for t in range(nt):
+            for hh in range(2):
+                for g, u in halves_of(n + 1 - hh, OFF_BT):
+                    src_f = loaded[(g, "bs")][:].bitcast(F32).rearrange("p (t w) -> p t w", t=4)
+                    if hh == 0:
+                        pb = bank("pb", "tm", 2)
+                        tmb[(g, u)] = pb
+                    pbv = tmb[(g, u)][:].rearrange("q (t i) -> q t i", t=4)
+                    for t in (2 * hh, 2 * hh + 1):
                         nc.tensor.transpose(pbv[:, t, :], src_f[:, t, P * u : P * u + P], ident[:])
-                    tmb[(g, kind, u)] = pb[:].bitcast(BF16)[:, 0 : 2 * nt * P].rearrange("q (s e) -> q s e", e=2)
             k = unit_of(n, OFF_BK)
             bk = None
             if k is not None and k[1] < NTS[k[0]]:
                 g, t = k
-                bk = bank("bk", "tx", 4)
+                bk = bank("bk", "bk", 1)
                 bkv = bk[:].rearrange("i (j q) -> i j q", j=4)
                 for j in range(4):
                     nc.tensor.transpose(bkv[:, j, :], mts[(g, j)][:, t * P : (t + 1) * P], ident[:])
 
             for dst, srcv in s_copies:
                 nc.scalar.copy(out=dst, in_=srcv)
-            if bk is not None:
-                g, t = k
+            v = unit_of(n, OFF_V)
+            if v is not None:
+                g, j = v
+                vt = ep.tile([P, 512], F32, name="vt", tag="vt", bufs=VT_BUFS)
+                vts[(g, j)] = vt
+                bt = tmb[(g, j // 2)][:].bitcast(BF16).rearrange("q (s e) -> q s e", e=2)[:, :, j % 2]
+                nc.scalar.activation(out=vt[:], in_=bt, func=ACT.Identity, bias=mc[:, j : j + 1], scale=md[:, j : j + 1])
+            z2 = unit_of(n, OFF_Z2)
+            if z2 is not None:
+                g, j = z2
+                mt = mts[(g, j)]
+                nc.scalar.activation(out=mt[:], in_=mt[:], func=ACT.Identity, bias=k0[:, j : j + 1])
+
+            back = bk_at.get(n - 1)
+            quantises(n)
+            z = unit_of(n, OFF_Z)
+            vt = None
+            if z is not None:
+                g, j = z
+                mt = ep.tile([P, 512], F32, name="mt", tag="mt", bufs=14)
+                mts[(g, j)] = mt
+                vt = vts[(g, j)]
+                spk4 = gr[(g, 3)][:].rearrange("q (s t) -> q s t", t=4)
+                nc.vector.tensor_tensor(out=mt[:], in0=vt[:], in1=spk4[:, :, j], op=ALU.mult)
+            i = n + MN_LEAD - OFF_BK - 1
+            if 0 <= i < 4 * G:
+                make_mn(i, vt)
+            if back is not None:
+                g, t, pbk = back
                 nt = NTS[g]
                 ob = ep.tile([P, R_IN], F32, name="ob", tag="ob", bufs=8)
-                nc.scalar.copy(
+                nc.vector.tensor_tensor(
                     out=ob[:].rearrange("i (u q e) -> i u q e", u=2, q=P, e=2),
-                    in_=bk[:].rearrange("i (u e q) -> i u q e", u=2, e=2, q=P),
+                    in0=pbk[:].rearrange("i (u e q) -> i u q e", u=2, e=2, q=P),
+                    in1=mns[4 * g + t].rearrange("i (u q e) -> i u q e", u=2, q=P, e=2),
+                    op=ALU.add,
                 )
                 nc.sync.dma_start(
                     out=out[base[g] : base[g] + nt * P, :].rearrange("(p t) n -> p t n", t=nt)[:, t, :], in_=ob[:]
                 )
-            for g, u in halves_of(n, OFF_Y1):
-                ns = P * NTS[g]
-                spk4 = gr[(g, 3)][:, 0 : 4 * ns].rearrange("q (s t) -> q s t", t=4)
-                for j in (2 * u, 2 * u + 1):
-                    yt = ep.tile([P, 512], F32, name="yt", tag="yt", bufs=8)
-                    yts[(g, j)] = yt
-                    nc.scalar.activation(
-                        out=yt[:, 0:ns], in_=spk4[:, :, j], func=ACT.Identity, bias=k0[:, j : j + 1], scale=mc[:, j : j + 1]
-                    )
-
+            if bk is not None:
+                bk_at[n] = (k[0], k[1], bk)
             prev = mx_at.get(n - 1)
             if prev is not None:
                 g, j, acc = prev
@@ -265,44 +314,6 @@ def tile_snnlayer_pa_t_kernel(
                 nc.vector.scalar_tensor_tensor(
                     out=mt[:, 0:ns], in0=acc[:, 0:ns], scalar=c3[:, j : j + 1], in1=mt[:, 0:ns], op0=ALU.mult, op1=ALU.add
                 )
-            if mem_now:
-                quantises(n)
-            for g, u in bt_now:
-                ns = P * NTS[g]
-                for e in range(2):
-                    j = 2 * u + e
-                    mt = ep.tile([P, 512], F32, name="mt", tag="mt", bufs=14)
-                    mts[(g, j)] = mt
-                    nc.vector.scalar_tensor_tensor(
-                        out=mt[:, 0:ns],
-                        in0=tmb[(g, "b", u)][:, :, e],
-                        scalar=md[:, j : j + 1],
-                        in1=yts[(g, j)][:, 0:ns],
-                        op0=ALU.mult,
-                        op1=ALU.add,
-                    )
-            for g, u in halves_of(n, OFF_BS):
-                nt = NTS[g]
-                bv = loaded[(g, "bs")][:, 0 : nt * 512].rearrange("p (t k) -> p t k", t=nt)[:, :, 256 * u : 256 * u + 256]
-                sv = loaded[(g, "ss")][:, 0 : nt * 1024].rearrange("p (t k) -> p t k", t=nt)[:, :, 512 + 256 * u : 768 + 256 * u]
-                pv = loaded[(g, "ms")][:, 0 : nt * 512].rearrange("p (t k) -> p t k", t=nt)[:, :, 256 * u : 256 * u + 256]
-                for t in range(nt):
-                    nc.gpsimd.tensor_tensor(out=pv[:, t, :], in0=bv[:, t, :], in1=sv[:, t, :], op=ALU.mult)
-            for g, u in mem_now:
-                ns = P * NTS[g]
-                for e in range(2):
-                    j = 2 * u + e
-                    yt = yts[(g, j)]
-                    nc.vector.scalar_tensor_tensor(
-                        out=yt[:, 0:ns],
-                        in0=tmb[(g, "m", u)][:, :, e],
-                        scalar=aa[:, j : j + 1],
-                        in1=yt[:, 0:ns],
-                        op0=ALU.mult,
-                        op1=ALU.add,
-                    )
-            if not mem_now:
-                quantises(n)
 
             m = unit_of(n, OFF_MX)
             if m is not None:

@@ -15,51 +15,31 @@ P = 128
 B, IN_DIM, R_IN = 4096, 1024, 512
 FLOPS = 2 * B * (IN_DIM + 2 * R_IN) * R_IN
 
-NTS = (4, 4, 4, 4, 4, 4, 4, 4)
-G = len(NTS)
+NT = 2
+NS = NT * P
+G = B // NS
 PASS_ORDER = (3, 2, 0, 1)
-OFF_BT = (1, 3)
-OFF_V = 1
-OFF_Z = 2
-OFF_Z2 = 3
-OFF_Q = 1
-OFF_MX = 5
-OFF_BK = 10
-MN_LEAD = 3
-VT_BUFS = 8
-N_UNITS = 4 * G + OFF_BK + 4
-PINNED = True
-SPLIT_GROUPS = 2
-assert sum(NTS) * P == B
-
-
-def unit_of(n, off):
-    d = n - off
-    if d >= 0 and d // 4 < G:
-        return (d // 4, d % 4)
-    return None
-
-
-def halves_of(n, offs):
-    res = []
-    for u in range(2):
-        d = n - offs[u]
-        if d >= 0 and d % 4 == 0 and d // 4 < G:
-            res.append((d // 4, u))
-    return res
+AHEAD = 4
+OFF_V = 0
+OFF_Z = 1
+OFF_Z2 = 2
+OFF_MX = 2
+OFF_BK = 5
+MN_LEAD = 4
+A_UNIT = 1
+WX_UNIT = 1
+N_UNITS = 2 * (G - 1) + OFF_BK + 3
 
 
 def tile_snnlayer_pa_t_kernel(
     tc, x_t, spk_t, mem_t_in, b_t_in, W_x2in, b_x2in, W_rec4in, b_rec4in, W_out2in, b_out2in, tau_adp_in, tau_m_in, out
 ):
     nc = tc.nc
-    base = [P * sum(NTS[:g]) for g in range(G)]
     with ExitStack() as ctx:
-        if PINNED:
-            ctx.enter_context(tc.manual_schedule())
+        ctx.enter_context(tc.manual_schedule())
         const = ctx.enter_context(tc.tile_pool(name="const", bufs=1))
-        ld = ctx.enter_context(tc.tile_pool(name="ld", bufs=3))
-        qp = ctx.enter_context(tc.tile_pool(name="qp", bufs=2))
+        ld = ctx.enter_context(tc.tile_pool(name="ld", bufs=AHEAD + 2))
+        qp = ctx.enter_context(tc.tile_pool(name="qp", bufs=3))
         ep = ctx.enter_context(tc.tile_pool(name="ep", bufs=2))
         ps = ctx.enter_context(tc.psum_pool(name="ps", bufs=1))
 
@@ -72,34 +52,41 @@ def tile_snnlayer_pa_t_kernel(
         def load(g, names):
             if g >= G:
                 return
-            nt = NTS[g]
             for nm in names:
                 src, width = srcs[nm]
-                dst = ld.tile([P, 4 * width], BF16, name=nm, tag=nm)
-                dst_v = dst[:, 0 : nt * width].rearrange("p (t k) -> p t k", t=nt)
-                src_v = src[base[g] : base[g] + nt * P, :].rearrange("(p t) k -> p t k", t=nt)
-                if g < SPLIT_GROUPS:
-                    for h in range(2):
-                        nc.sync.dma_start(out=dst_v[:, 2 * h : 2 * h + 2, :], in_=src_v[:, 2 * h : 2 * h + 2, :])
-                else:
-                    nc.sync.dma_start(out=dst_v, in_=src_v)
+                dst = ld.tile([P, NT, width], BF16, name=nm, tag=nm)
+                nc.sync.dma_start(out=dst[:], in_=src[g * NS : (g + 1) * NS, :].rearrange("(p t) k -> p t k", t=NT))
                 loaded[(g, nm)] = dst
+
+        def words(g, nm):
+            width = srcs[nm][1]
+            return loaded[(g, nm)][:].rearrange("p t k -> p (t k)").bitcast(F32).rearrange("p (t w) -> p t w", t=NT)
 
         craw = const.tile([P, 256], BF16, name="craw")
         nc.vector.memset(craw[:], 0.0)
         ident = const.tile([P, P], F32, name="ident")
         make_identity(nc, ident[:])
+        wro = const.tile([P, 4096], BF16, name="wro")
+        wx = const.tile([P, 4096], BF16, name="wx")
 
-        wro = ld.tile([P, 4096], BF16, name="wro", tag="ss")
-        wx = ld.tile([P, 4096], BF16, name="wx", tag="xs")
-        for wi, (dst, src) in enumerate(((wro[:, 0:2048], W_rec4in), (wro[:, 2048:4096], W_out2in), (wx[:], W_x2in))):
+        def w_load(dst, src):
             dst_v = dst.rearrange("p (u e k) -> p u e k", u=2, e=2)
             src_v = src.rearrange("(u p e) k -> p u e k", u=2, p=P, e=2)
             for u in range(2):
                 nc.sync.dma_start(out=dst_v[:, u], in_=src_v[:, u])
-            if wi == 0:
-                for v, vec in enumerate((b_x2in, b_rec4in, b_out2in, tau_adp_in, tau_m_in)):
-                    nc.sync.dma_start(out=craw[2 * v : 2 * v + 2, :], in_=vec.rearrange("(u w) -> u w", u=2))
+
+        w_load(wro[:, 0:2048], W_rec4in)
+        for v, vec in enumerate((b_x2in, b_rec4in, b_out2in, tau_adp_in, tau_m_in)):
+            nc.sync.dma_start(out=craw[2 * v : 2 * v + 2, :], in_=vec.rearrange("(u w) -> u w", u=2))
+        w_load(wro[:, 2048:4096], W_out2in)
+        load(0, ("ss", "bs"))
+        w_load(wx[:], W_x2in)
+        load(0, ("xs",))
+        load(1, ("ss", "bs", "xs"))
+        load(0, ("ms",))
+        for g in range(2, AHEAD):
+            load(g, ("ss", "bs", "xs"))
+            load(g - 1, ("ms",))
 
         cst = const.tile([P, 20], F32, name="cst")
         bsum = const.tile([P, 4], F32, name="bsum")
@@ -110,6 +97,7 @@ def tile_snnlayer_pa_t_kernel(
         c3 = const.tile([P, 4], F32, name="c3")
         k0 = const.tile([P, 4], F32, name="k0")
         aa = sg[:, 4:8]
+        a_nat = const.tile([P, R_IN], F32, name="a_nat")
 
         def make_constants():
             cps = bank("cps", "tx", 3)
@@ -124,13 +112,11 @@ def tile_snnlayer_pa_t_kernel(
             nc.scalar.mul(out=c3[:], in_=ng[:, 4:8], mul=3.0)
             nc.vector.tensor_mul(out=k0[:], in0=c3[:], in1=bsum[:])
 
-        a_nat = const.tile([P, R_IN], F32, name="a_nat")
-
         def make_a_nat():
-            aps = bank("aps", "tx", 3)
+            aps = bank("aps", "bk", 2)
             for j in range(4):
                 nc.tensor.transpose(aps[:, j * P : (j + 1) * P], aa[:, j : j + 1].to_broadcast([P, P]), ident[:])
-            nc.scalar.copy(
+            nc.vector.tensor_copy(
                 out=a_nat[:].rearrange("i (u q e) -> i u q e", u=2, q=P, e=2),
                 in_=aps[:].rearrange("i (u e q) -> i u q e", u=2, e=2, q=P),
             )
@@ -147,25 +133,7 @@ def tile_snnlayer_pa_t_kernel(
             lo = (0 if c == 3 else 1024) + j * 256 + P * u
             return wro_f[:, lo : lo + P]
 
-        gr = {}
-        ac = {}
-        vts = {}
-        mts = {}
-        tmb = {}
-        mx_at = {}
-        bk_at = {}
-        mns = {}
         gws = {}
-
-        def make_mn(i, grt):
-            if grt is None:
-                mn = ep.tile([P, R_IN], F32, name="mn", tag="mn", bufs=4)
-                mn = mn[:]
-            else:
-                mn = grt[:]
-            mns[i] = mn
-            mv = loaded[(i // 4, "ms")][:].rearrange("p (t k) -> p t k", t=4)
-            nc.gpsimd.tensor_tensor(out=mn, in0=mv[:, i % 4, :], in1=a_nat[:], op=ALU.mult)
 
         def w_quantise(ci):
             nc.vector.quantize_mx(
@@ -174,11 +142,9 @@ def tile_snnlayer_pa_t_kernel(
                 in_=gws[ci][:],
             )
 
-        load(0, ("ss", "xs", "bs"))
-        load(1, ("ss", "xs", "bs"))
-        load(0, ("ms",))
-        for ci, c in enumerate(PASS_ORDER):
-            gw = qp.tile([P, 2048], BF16, name="gw%d" % c, tag="gr%d" % c, align_bytes=64)
+        def weights(ci):
+            c = PASS_ORDER[ci]
+            gw = qp.tile([P, 2048], BF16, name="gw", tag="gr%d" % (ci // 2), align_bytes=64)
             gws[ci] = gw
             gw_f = gw[:].bitcast(F32).rearrange("q (m n u) -> q m n u", m=4, n=P, u=2)
             for jj in range(2):
@@ -193,143 +159,154 @@ def tile_snnlayer_pa_t_kernel(
                     nc.scalar.copy(out=dst, in_=srcv)
                 else:
                     nc.vector.tensor_copy(out=dst, in_=srcv)
-            if ci == 0:
-                make_constants()
-            else:
-                w_quantise(ci - 1)
-        w_quantise(3)
-        make_a_nat()
-        load(2, ("ss", "xs", "bs"))
-        load(1, ("ms",))
 
-        def quantises(n):
-            q = unit_of(n, OFF_Q)
-            if q is not None:
-                g, r = q
-                c = PASS_ORDER[r]
-                ns = P * NTS[g]
-                a_c = qp.tile([P, 512], U32, name="ac%d" % c, tag="ac%d" % c, bufs=3, align_bytes=64)
-                a_s = qp.tile([P, 512], U8, name="as%d" % c, tag="as%d" % c, bufs=3, align_bytes=64)
-                nc.vector.quantize_mx(out=a_c[:, 0:ns].bitcast(FP8X4), scales=a_s[:, 0:ns], in_=gr[(g, c)][:, 0 : 4 * ns])
-                ac[(g, c)] = (a_c, a_s)
+        weights(0)
+        make_constants()
+        weights(1)
+        w_quantise(0)
+        w_quantise(1)
+
+        gr, ac, accs, tmb, vts, mts, mns, bks = {}, {}, {}, {}, {}, {}, {}, {}
 
         for n in range(N_UNITS):
-            if n % 4 == 0 and n > 0:
-                load(n // 4 + 2, ("ss", "xs"))
-            elif n % 4 == 3 and n > 3:
-                load(n // 4 + 2, ("bs",))
-            if n % 4 == 1 and n // 4 >= 2:
-                load(n // 4, ("ms",))
+            def at(age):
+                d = n - age
+                return (d // 2, d % 2) if 0 <= d < 2 * G else None
 
-            s_copies = []
-            a = unit_of(n, 0)
-            if a is not None:
-                g, r = a
-                c = PASS_ORDER[r]
-                nt = NTS[g]
-                tf = min(nt, 2)
-                nf = nt // tf
-                src_t = loaded[(g, "xs" if c < 2 else "ss")]
-                src_f = src_t[:].bitcast(F32)[:, 0 : nt * 512].rearrange("p (t w) -> p t w", t=nt)
-                woff = 256 * (c % 2)
-                grt = qp.tile([P, 2048], BF16, name="gr%d" % c, tag="gr%d" % c, align_bytes=64)
-                gr[(g, c)] = grt
-                gr_f = grt[:].bitcast(F32)[:, 0 : nt * 256].rearrange("q (h t i u) -> q h t i u", h=nf, t=tf, i=P, u=2)
-                for h in range(nf):
-                    pt = bank("xt", "tx", 3)
-                    ptv = pt[:, 0 : tf * 256].rearrange("q (t u i) -> q t u i", t=tf, u=2, i=P)
-                    for t2 in range(tf):
-                        for u in range(2):
-                            nc.tensor.transpose(
-                                ptv[:, t2, u, :], src_f[:, tf * h + t2, woff + P * u : woff + P * u + P], ident[:]
-                            )
-                    s_copies.append((gr_f[:, h], ptv.rearrange("q t u i -> q t i u")))
-            for hh in range(2):
-                for g, u in halves_of(n + 1 - hh, OFF_BT):
-                    src_f = loaded[(g, "bs")][:].bitcast(F32).rearrange("p (t w) -> p t w", t=4)
-                    if hh == 0:
-                        pb = bank("pb", "tm", 2)
-                        tmb[(g, u)] = pb
-                    pbv = tmb[(g, u)][:].rearrange("q (t i) -> q t i", t=4)
-                    for t in (2 * hh, 2 * hh + 1):
-                        nc.tensor.transpose(pbv[:, t, :], src_f[:, t, P * u : P * u + P], ident[:])
-            k = unit_of(n, OFF_BK)
-            bk = None
-            if k is not None and k[1] < NTS[k[0]]:
-                g, t = k
-                bk = bank("bk", "bk", 1)
-                bkv = bk[:].rearrange("i (j q) -> i j q", j=4)
-                for j in range(4):
-                    nc.tensor.transpose(bkv[:, j, :], mts[(g, j)][:, t * P : (t + 1) * P], ident[:])
+            if n % 2 == 0:
+                load(n // 2 + AHEAD, ("ss", "bs"))
+            else:
+                load(n // 2 + AHEAD, ("xs",))
+                load(n // 2 + AHEAD - 1, ("ms",))
 
-            for dst, srcv in s_copies:
-                nc.scalar.copy(out=dst, in_=srcv)
-            v = unit_of(n, OFF_V)
-            if v is not None:
-                g, j = v
-                vt = ep.tile([P, 512], F32, name="vt", tag="vt", bufs=VT_BUFS)
-                vts[(g, j)] = vt
-                bt = tmb[(g, j // 2)][:].bitcast(BF16).rearrange("q (s e) -> q s e", e=2)[:, :, j % 2]
-                nc.scalar.activation(out=vt[:], in_=bt, func=ACT.Identity, bias=mc[:, j : j + 1], scale=md[:, j : j + 1])
-            z2 = unit_of(n, OFF_Z2)
-            if z2 is not None:
-                g, j = z2
-                mt = mts[(g, j)]
-                nc.scalar.activation(out=mt[:], in_=mt[:], func=ACT.Identity, bias=k0[:, j : j + 1])
+            if n == WX_UNIT:
+                weights(2)
+                weights(3)
+                w_quantise(2)
+                w_quantise(3)
+            if n == A_UNIT:
+                make_a_nat()
 
-            back = bk_at.get(n - 1)
-            quantises(n)
-            z = unit_of(n, OFF_Z)
+            if at(1):
+                g, h = at(1)
+                a_c = qp.tile([P, 2 * NS], U32, name="ac%d" % h, tag="ac%d" % h, align_bytes=64)
+                a_s = qp.tile([P, 2 * NS], U8, name="as%d" % h, tag="as%d" % h, align_bytes=64)
+                nc.vector.quantize_mx(out=a_c[:].bitcast(FP8X4), scales=a_s[:], in_=gr[(g, h)][:])
+                ac[(g, h)] = (a_c, a_s)
             vt = None
-            if z is not None:
-                g, j = z
-                mt = ep.tile([P, 512], F32, name="mt", tag="mt", bufs=14)
-                mts[(g, j)] = mt
-                vt = vts[(g, j)]
-                spk4 = gr[(g, 3)][:].rearrange("q (s t) -> q s t", t=4)
-                nc.vector.tensor_tensor(out=mt[:], in0=vt[:], in1=spk4[:, :, j], op=ALU.mult)
-            i = n + MN_LEAD - OFF_BK - 1
-            if 0 <= i < 4 * G:
-                make_mn(i, vt)
-            if back is not None:
-                g, t, pbk = back
-                nt = NTS[g]
+            if at(OFF_Z):
+                g, u = at(OFF_Z)
+                mt = ep.tile([P, 2, NS], F32, name="mt", tag="mt", bufs=8)
+                mts[(g, u)] = mt
+                vt = vts[(g, u)]
+                spk4 = gr[(g, 0)][:, 0 : 4 * NS].rearrange("q (s t) -> q s t", t=4)
+                for e in range(2):
+                    nc.vector.tensor_tensor(out=mt[:, e, :], in0=vt[:, e, :], in1=spk4[:, :, 2 * u + e], op=ALU.mult)
+            i = n - OFF_BK - 1 + MN_LEAD
+            if 0 <= i < 2 * G:
+                if vt is None:
+                    mn = ep.tile([P, R_IN], F32, name="mn", tag="mn", bufs=2)
+                    mn = mn[:]
+                else:
+                    mn = vt[:].rearrange("p e s -> p (e s)")
+                mns[i] = mn
+                nc.gpsimd.tensor_tensor(out=mn, in0=loaded[(i // 2, "ms")][:, i % 2, :], in1=a_nat[:], op=ALU.mult)
+
+            if at(OFF_BK + 1):
+                g, t = at(OFF_BK + 1)
                 ob = ep.tile([P, R_IN], F32, name="ob", tag="ob", bufs=8)
                 nc.vector.tensor_tensor(
                     out=ob[:].rearrange("i (u q e) -> i u q e", u=2, q=P, e=2),
-                    in0=pbk[:].rearrange("i (u e q) -> i u q e", u=2, e=2, q=P),
-                    in1=mns[4 * g + t].rearrange("i (u q e) -> i u q e", u=2, q=P, e=2),
+                    in0=bks[(g, t)][:].rearrange("i (u e q) -> i u q e", u=2, e=2, q=P),
+                    in1=mns[2 * g + t].rearrange("i (u q e) -> i u q e", u=2, q=P, e=2),
                     op=ALU.add,
                 )
                 nc.sync.dma_start(
-                    out=out[base[g] : base[g] + nt * P, :].rearrange("(p t) n -> p t n", t=nt)[:, t, :], in_=ob[:]
+                    out=out[g * NS : (g + 1) * NS, :].rearrange("(p t) n -> p t n", t=NT)[:, t, :], in_=ob[:]
                 )
-            if bk is not None:
-                bk_at[n] = (k[0], k[1], bk)
-            prev = mx_at.get(n - 1)
-            if prev is not None:
-                g, j, acc = prev
-                ns = P * NTS[g]
-                mt = mts[(g, j)]
-                nc.vector.scalar_tensor_tensor(
-                    out=mt[:, 0:ns], in0=acc[:, 0:ns], scalar=c3[:, j : j + 1], in1=mt[:, 0:ns], op0=ALU.mult, op1=ALU.add
-                )
-
-            m = unit_of(n, OFF_MX)
-            if m is not None:
-                g, j = m
-                ns = P * NTS[g]
-                acc = bank("acc", "mx", 2)
-                for ci, c in enumerate(PASS_ORDER):
-                    a_c, a_s = ac[(g, c)]
-                    s0 = (ci * 4 + j) * P
-                    nc.tensor.matmul_mx(
-                        out=acc[:, 0:ns],
-                        lhsT=wcodes[:, s0 : s0 + P].bitcast(FP8X4),
-                        lhsT_scale=wscales[:, s0 : s0 + P],
-                        rhs=a_c[:, 0:ns].bitcast(FP8X4),
-                        rhs_scale=a_s[:, 0:ns],
-                        start=(ci == 0),
-                        stop=(ci == 3),
+            if at(OFF_MX + 1):
+                g, u = at(OFF_MX + 1)
+                mt = mts[(g, u)]
+                for e in range(2):
+                    j = 2 * u + e
+                    nc.vector.scalar_tensor_tensor(
+                        out=mt[:, e, :],
+                        in0=accs[(g, u)][:, e * NS : (e + 1) * NS],
+                        scalar=c3[:, j : j + 1],
+                        in1=mt[:, e, :],
+                        op0=ALU.mult,
+                        op1=ALU.add,
                     )
-                mx_at[n] = (g, j, acc)
+
+            s_copies = []
+            if at(0):
+                g, h = at(0)
+                grt = qp.tile([P, 2 * 4 * NS], BF16, name="gr%d" % h, tag="gr%d" % h, align_bytes=64)
+                gr[(g, h)] = grt
+                for c2 in range(2):
+                    c = PASS_ORDER[2 * h + c2]
+                    src_f = words(g, "xs" if c < 2 else "ss")
+                    woff = 256 * (c % 2)
+                    pt = bank("xt", "tx", 3)
+                    ptv = pt[:].rearrange("q (t u i) -> q t u i", t=NT, u=2, i=P)
+                    for t in range(NT):
+                        for u in range(2):
+                            nc.tensor.transpose(ptv[:, t, u, :], src_f[:, t, woff + P * u : woff + P * u + P], ident[:])
+                    s_copies.append(
+                        (
+                            grt[:].bitcast(F32)[:, c2 * 512 : (c2 + 1) * 512].rearrange("q (t i u) -> q t i u", t=NT, i=P, u=2),
+                            ptv.rearrange("q t u i -> q t i u"),
+                        )
+                    )
+            if at(OFF_V):
+                g, u = at(OFF_V)
+                pb = bank("pb", "tm", 1)
+                for t in range(NT):
+                    nc.tensor.transpose(pb[:, t * P : (t + 1) * P], words(g, "bs")[:, t, P * u : P * u + P], ident[:])
+                tmb[(g, u)] = pb
+            if at(OFF_BK):
+                g, t = at(OFF_BK)
+                bk = bank("bk", "bk", 2)
+                bkv = bk[:].rearrange("i (j q) -> i j q", j=4)
+                for j in range(4):
+                    nc.tensor.transpose(bkv[:, j, :], mts[(g, j // 2)][:, j % 2, t * P : (t + 1) * P], ident[:])
+                bks[(g, t)] = bk
+
+            if at(OFF_MX):
+                g, u = at(OFF_MX)
+                acc = bank("acc", "mx", 2)
+                accs[(g, u)] = acc
+                for e in range(2):
+                    j = 2 * u + e
+                    for ci in range(4):
+                        a_c, a_s = ac[(g, ci // 2)]
+                        o = (ci % 2) * NS
+                        w0 = (ci * 4 + j) * P
+                        nc.tensor.matmul_mx(
+                            out=acc[:, e * NS : (e + 1) * NS],
+                            lhsT=wcodes[:, w0 : w0 + P].bitcast(FP8X4),
+                            lhsT_scale=wscales[:, w0 : w0 + P],
+                            rhs=a_c[:, o : o + NS].bitcast(FP8X4),
+                            rhs_scale=a_s[:, o : o + NS],
+                            start=(ci == 0),
+                            stop=(ci == 3),
+                        )
+
+            for dst, srcv in s_copies:
+                nc.scalar.copy(out=dst, in_=srcv)
+            if at(OFF_V):
+                g, u = at(OFF_V)
+                vt = ep.tile([P, 2, NS], F32, name="vt", tag="vt", bufs=MN_LEAD + 3)
+                vts[(g, u)] = vt
+                btv = tmb[(g, u)][:, 0:NS].bitcast(BF16).rearrange("q (s e) -> q s e", e=2)
+                for e in range(2):
+                    j = 2 * u + e
+                    nc.scalar.activation(
+                        out=vt[:, e, :], in_=btv[:, :, e], func=ACT.Identity, bias=mc[:, j : j + 1], scale=md[:, j : j + 1]
+                    )
+            if at(OFF_Z2):
+                g, u = at(OFF_Z2)
+                mt = mts[(g, u)]
+                for e in range(2):
+                    j = 2 * u + e
+                    nc.scalar.activation(out=mt[:, e, :], in_=mt[:, e, :], func=ACT.Identity, bias=k0[:, j : j + 1])

@@ -20,12 +20,12 @@ NS = NT * P
 G = B // NS
 PASS_ORDER = (3, 2, 0, 1)
 AHEAD = 4
-OFF_V = 0
-OFF_Z = 1
-OFF_Z2 = 2
+OFF_Z = 0
+OFF_Z2 = 1
 OFF_MX = 2
 OFF_BK = 5
 MN_LEAD = 4
+GR_BUFS = 4
 A_UNIT = 1
 WX_UNIT = 1
 N_UNITS = 2 * (G - 1) + OFF_BK + 3
@@ -39,7 +39,7 @@ def tile_snnlayer_pa_t_kernel(
         ctx.enter_context(tc.manual_schedule())
         const = ctx.enter_context(tc.tile_pool(name="const", bufs=1))
         ld = ctx.enter_context(tc.tile_pool(name="ld", bufs=AHEAD + 2))
-        qp = ctx.enter_context(tc.tile_pool(name="qp", bufs=3))
+        qp = ctx.enter_context(tc.tile_pool(name="qp", bufs=GR_BUFS))
         ep = ctx.enter_context(tc.tile_pool(name="ep", bufs=2))
         ps = ctx.enter_context(tc.psum_pool(name="ps", bufs=1))
 
@@ -94,6 +94,8 @@ def tile_snnlayer_pa_t_kernel(
         ng = const.tile([P, 8], F32, name="ng")
         md = const.tile([P, 4], F32, name="md")
         mc = const.tile([P, 4], F32, name="mc")
+        dd = const.tile([P, 4], F32, name="dd")
+        rr = const.tile([P, 4], F32, name="rr")
         c3 = const.tile([P, 4], F32, name="c3")
         k0 = const.tile([P, 4], F32, name="k0")
         aa = sg[:, 4:8]
@@ -107,8 +109,11 @@ def tile_snnlayer_pa_t_kernel(
             nc.vector.tensor_add(out=bsum[:], in0=bsum[:], in1=cst[:, 8:12])
             nc.scalar.activation(out=sg[:], in_=cst[:, 12:20], func=ACT.Sigmoid)
             nc.scalar.activation(out=ng[:], in_=cst[:, 12:20], func=ACT.Sigmoid, scale=-1.0)
-            nc.vector.tensor_scalar(out=mc[:], in0=ng[:, 0:4], scalar1=-1.8, scalar2=-0.1, op0=ALU.mult, op1=ALU.add)
-            nc.scalar.mul(out=md[:], in_=sg[:, 0:4], mul=-1.8)
+            nc.vector.tensor_scalar(out=mc[:], in0=ng[:, 0:4], scalar1=1.8, scalar2=0.1, op0=ALU.mult, op1=ALU.add)
+            nc.vector.tensor_scalar(out=dd[:], in0=sg[:, 0:4], scalar1=1.8, scalar2=1e-30, op0=ALU.mult, op1=ALU.max)
+            nc.scalar.mul(out=md[:], in_=dd[:], mul=-1.0)
+            nc.vector.reciprocal(out=rr[:], in_=dd[:])
+            nc.vector.tensor_mul(out=rr[:], in0=mc[:], in1=rr[:])
             nc.scalar.mul(out=c3[:], in_=ng[:, 4:8], mul=3.0)
             nc.vector.tensor_mul(out=k0[:], in0=c3[:], in1=bsum[:])
 
@@ -166,7 +171,7 @@ def tile_snnlayer_pa_t_kernel(
         w_quantise(0)
         w_quantise(1)
 
-        gr, ac, accs, tmb, vts, mts, mns, bks = {}, {}, {}, {}, {}, {}, {}, {}
+        gr, ac, accs, tmb, mts, mns, bks = {}, {}, {}, {}, {}, {}, {}
 
         for n in range(N_UNITS):
             def at(age):
@@ -193,22 +198,13 @@ def tile_snnlayer_pa_t_kernel(
                 a_s = qp.tile([P, 2 * NS], U8, name="as%d" % h, tag="as%d" % h, align_bytes=64)
                 nc.vector.quantize_mx(out=a_c[:].bitcast(FP8X4), scales=a_s[:], in_=gr[(g, h)][:])
                 ac[(g, h)] = (a_c, a_s)
-            vt = None
-            if at(OFF_Z):
-                g, u = at(OFF_Z)
-                mt = ep.tile([P, 2, NS], F32, name="mt", tag="mt", bufs=8)
-                mts[(g, u)] = mt
-                vt = vts[(g, u)]
-                spk4 = gr[(g, 0)][:, 0 : 4 * NS].rearrange("q (s t) -> q s t", t=4)
-                for e in range(2):
-                    nc.vector.tensor_tensor(out=mt[:, e, :], in0=vt[:, e, :], in1=spk4[:, :, 2 * u + e], op=ALU.mult)
             i = n - OFF_BK - 1 + MN_LEAD
             if 0 <= i < 2 * G:
-                if vt is None:
+                if at(1):
+                    mn = gr[at(1)][:, 4 * NS : 8 * NS].bitcast(F32)
+                else:
                     mn = ep.tile([P, R_IN], F32, name="mn", tag="mn", bufs=2)
                     mn = mn[:]
-                else:
-                    mn = vt[:].rearrange("p e s -> p (e s)")
                 mns[i] = mn
                 nc.gpsimd.tensor_tensor(out=mn, in0=loaded[(i // 2, "ms")][:, i % 2, :], in1=a_nat[:], op=ALU.mult)
 
@@ -258,8 +254,8 @@ def tile_snnlayer_pa_t_kernel(
                             ptv.rearrange("q t u i -> q t i u"),
                         )
                     )
-            if at(OFF_V):
-                g, u = at(OFF_V)
+            if at(OFF_Z):
+                g, u = at(OFF_Z)
                 pb = bank("pb", "tm", 1)
                 for t in range(NT):
                     nc.tensor.transpose(pb[:, t * P : (t + 1) * P], words(g, "bs")[:, t, P * u : P * u + P], ident[:])
@@ -294,19 +290,21 @@ def tile_snnlayer_pa_t_kernel(
 
             for dst, srcv in s_copies:
                 nc.scalar.copy(out=dst, in_=srcv)
-            if at(OFF_V):
-                g, u = at(OFF_V)
-                vt = ep.tile([P, 2, NS], F32, name="vt", tag="vt", bufs=MN_LEAD + 3)
-                vts[(g, u)] = vt
-                btv = tmb[(g, u)][:, 0:NS].bitcast(BF16).rearrange("q (s e) -> q s e", e=2)
-                for e in range(2):
-                    j = 2 * u + e
-                    nc.scalar.activation(
-                        out=vt[:, e, :], in_=btv[:, :, e], func=ACT.Identity, bias=mc[:, j : j + 1], scale=md[:, j : j + 1]
-                    )
             if at(OFF_Z2):
                 g, u = at(OFF_Z2)
                 mt = mts[(g, u)]
                 for e in range(2):
                     j = 2 * u + e
-                    nc.scalar.activation(out=mt[:, e, :], in_=mt[:, e, :], func=ACT.Identity, bias=k0[:, j : j + 1])
+                    nc.scalar.activation(out=mt[:, e, :], in_=mt[:, e, :], func=ACT.Identity, bias=k0[:, j : j + 1], scale=md[:, j : j + 1])
+
+            if at(OFF_Z):
+                g, u = at(OFF_Z)
+                mt = ep.tile([P, 2, NS], F32, name="mt", tag="mt", bufs=8)
+                mts[(g, u)] = mt
+                btv = tmb[(g, u)][:, 0:NS].bitcast(BF16).rearrange("q (s e) -> q s e", e=2)
+                spk4 = gr[(g, 0)][:, 0 : 4 * NS].rearrange("q (s t) -> q s t", t=4)
+                for e in range(2):
+                    j = 2 * u + e
+                    nc.vector.scalar_tensor_tensor(
+                        out=mt[:, e, :], in0=btv[:, :, e], scalar=rr[:, j : j + 1], in1=spk4[:, :, j], op0=ALU.add, op1=ALU.mult
+                    )

@@ -19,14 +19,13 @@ NT = 2
 NS = NT * P
 G = B // NS
 PASS_ORDER = (3, 2, 0, 1)
-AHEAD = 4
-OFF_Z = 0
-OFF_Z2 = 1
+OFF_Z = 1
+OFF_Z2 = 2
 OFF_MX = 2
 OFF_BK = 5
 MN_LEAD = 4
 GR_BUFS = 4
-A_UNIT = 1
+A_UNIT = 2
 WX_UNIT = 1
 N_UNITS = 2 * (G - 1) + OFF_BK + 3
 
@@ -38,7 +37,7 @@ def tile_snnlayer_pa_t_kernel(
     with ExitStack() as ctx:
         ctx.enter_context(tc.manual_schedule())
         const = ctx.enter_context(tc.tile_pool(name="const", bufs=1))
-        ld = ctx.enter_context(tc.tile_pool(name="ld", bufs=AHEAD + 2))
+        ld = ctx.enter_context(tc.tile_pool(name="ld", bufs=3))
         qp = ctx.enter_context(tc.tile_pool(name="qp", bufs=GR_BUFS))
         ep = ctx.enter_context(tc.tile_pool(name="ep", bufs=2))
         ps = ctx.enter_context(tc.psum_pool(name="ps", bufs=1))
@@ -49,18 +48,20 @@ def tile_snnlayer_pa_t_kernel(
         srcs = {"ss": (spk_t, 1024), "xs": (x_t, 1024), "bs": (b_t_in, 512), "ms": (mem_t_in, 512)}
         loaded = {}
 
-        def load(g, names):
-            if g >= G:
+        def load(pair, nm, part=None):
+            if 2 * pair >= G:
                 return
-            for nm in names:
-                src, width = srcs[nm]
-                dst = ld.tile([P, NT, width], BF16, name=nm, tag=nm)
-                nc.sync.dma_start(out=dst[:], in_=src[g * NS : (g + 1) * NS, :].rearrange("(p t) k -> p t k", t=NT))
-                loaded[(g, nm)] = dst
+            src, width = srcs[nm]
+            if part in (None, 0):
+                loaded[(pair, nm)] = ld.tile([P, 2 * NT, width], BF16, name=nm, tag=nm)
+            dst = loaded[(pair, nm)]
+            src_v = src[2 * pair * NS : 2 * (pair + 1) * NS, :].rearrange("(p t) k -> p t k", t=2 * NT)
+            lo, hi = (0, 2 * NT) if part is None else (part * NT, (part + 1) * NT)
+            nc.sync.dma_start(out=dst[:, lo:hi, :], in_=src_v[:, lo:hi, :])
 
         def words(g, nm):
-            width = srcs[nm][1]
-            return loaded[(g, nm)][:].rearrange("p t k -> p (t k)").bitcast(F32).rearrange("p (t w) -> p t w", t=NT)
+            v = loaded[(g // 2, nm)][:].rearrange("p t k -> p (t k)").bitcast(F32).rearrange("p (t w) -> p t w", t=2 * NT)
+            return v[:, (g % 2) * NT : (g % 2 + 1) * NT, :]
 
         craw = const.tile([P, 256], BF16, name="craw")
         nc.vector.memset(craw[:], 0.0)
@@ -79,14 +80,13 @@ def tile_snnlayer_pa_t_kernel(
         for v, vec in enumerate((b_x2in, b_rec4in, b_out2in, tau_adp_in, tau_m_in)):
             nc.sync.dma_start(out=craw[2 * v : 2 * v + 2, :], in_=vec.rearrange("(u w) -> u w", u=2))
         w_load(wro[:, 2048:4096], W_out2in)
-        load(0, ("ss", "bs"))
+        load(0, "ss", 0)
         w_load(wx[:], W_x2in)
-        load(0, ("xs",))
-        load(1, ("ss", "bs", "xs"))
-        load(0, ("ms",))
-        for g in range(2, AHEAD):
-            load(g, ("ss", "bs", "xs"))
-            load(g - 1, ("ms",))
+        for part in range(2):
+            for nm in ("xs", "bs", "ms") if part == 0 else ("ss", "xs", "bs", "ms"):
+                load(0, nm, part)
+        for nm in ("ss", "bs", "xs", "ms"):
+            load(1, nm)
 
         cst = const.tile([P, 20], F32, name="cst")
         bsum = const.tile([P, 4], F32, name="bsum")
@@ -160,7 +160,7 @@ def tile_snnlayer_pa_t_kernel(
                         nc.tensor.transpose(ptv[:, m2, u, :], w_words(c, 2 * jj + m2, u), ident[:])
                 dst = gw_f[:, 2 * jj : 2 * jj + 2, :, :]
                 srcv = ptv.rearrange("q m u n -> q m n u")
-                if jj == 0:
+                if jj == 0 or ci > 1:
                     nc.scalar.copy(out=dst, in_=srcv)
                 else:
                     nc.vector.tensor_copy(out=dst, in_=srcv)
@@ -171,18 +171,14 @@ def tile_snnlayer_pa_t_kernel(
         w_quantise(0)
         w_quantise(1)
 
-        gr, ac, accs, tmb, mts, mns, bks = {}, {}, {}, {}, {}, {}, {}
+        gr, ac, accs, tmb, mts, mns, bks, obs = {}, {}, {}, {}, {}, {}, {}, {}
 
         for n in range(N_UNITS):
             def at(age):
                 d = n - age
                 return (d // 2, d % 2) if 0 <= d < 2 * G else None
 
-            if n % 2 == 0:
-                load(n // 2 + AHEAD, ("ss", "bs"))
-            else:
-                load(n // 2 + AHEAD, ("xs",))
-                load(n // 2 + AHEAD - 1, ("ms",))
+            load(n // 4 + 2, ("ss", "bs", "xs", "ms")[n % 4])
 
             if n == WX_UNIT:
                 weights(2)
@@ -206,20 +202,23 @@ def tile_snnlayer_pa_t_kernel(
                     mn = ep.tile([P, R_IN], F32, name="mn", tag="mn", bufs=2)
                     mn = mn[:]
                 mns[i] = mn
-                nc.gpsimd.tensor_tensor(out=mn, in0=loaded[(i // 2, "ms")][:, i % 2, :], in1=a_nat[:], op=ALU.mult)
+                nc.gpsimd.tensor_tensor(out=mn, in0=loaded[(i // 4, "ms")][:, i % 4, :], in1=a_nat[:], op=ALU.mult)
 
             if at(OFF_BK + 1):
                 g, t = at(OFF_BK + 1)
-                ob = ep.tile([P, R_IN], F32, name="ob", tag="ob", bufs=8)
+                if t == 0:
+                    obs[g] = ep.tile([P, NT, R_IN], F32, name="ob", tag="ob", bufs=4)
+                ob = obs[g]
                 nc.vector.tensor_tensor(
-                    out=ob[:].rearrange("i (u q e) -> i u q e", u=2, q=P, e=2),
+                    out=ob[:, t, :].rearrange("i (u q e) -> i u q e", u=2, q=P, e=2),
                     in0=bks[(g, t)][:].rearrange("i (u e q) -> i u q e", u=2, e=2, q=P),
                     in1=mns[2 * g + t].rearrange("i (u q e) -> i u q e", u=2, q=P, e=2),
                     op=ALU.add,
                 )
-                nc.sync.dma_start(
-                    out=out[g * NS : (g + 1) * NS, :].rearrange("(p t) n -> p t n", t=NT)[:, t, :], in_=ob[:]
-                )
+                lo, hi = (t, t + 1) if g == G - 1 else (0, NT)
+                if t == NT - 1 or g == G - 1:
+                    out_v = out[2 * (g // 2) * NS : 2 * (g // 2 + 1) * NS, :].rearrange("(p t) n -> p t n", t=2 * NT)
+                    nc.sync.dma_start(out=out_v[:, (g % 2) * NT + lo : (g % 2) * NT + hi, :], in_=ob[:, lo:hi, :])
             if at(OFF_MX + 1):
                 g, u = at(OFF_MX + 1)
                 mt = mts[(g, u)]

@@ -25,6 +25,7 @@ OFF_MX = 2
 OFF_BK = 5
 MN_LEAD = 4
 GR_BUFS = 4
+WARM = (6, 2, 2, 1, 1, 1, 1, 1, 0)
 A_UNIT = 2
 WX_UNIT = 1
 N_UNITS = 2 * (G - 1) + OFF_BK + 3
@@ -67,6 +68,16 @@ def tile_snnlayer_pa_t_kernel(
         nc.vector.memset(craw[:], 0.0)
         ident = const.tile([P, P], F32, name="ident")
         make_identity(nc, ident[:])
+        zero = const.tile([P, 512], BF16, name="zero")
+        nc.vector.memset(zero[:], 0.0)
+
+        def keep_warm(count):
+            if count:
+                warm = bank("warm", "bk", 2)
+                for i in range(count):
+                    nc.tensor.matmul(warm[:], lhsT=zero[:, 0:P], rhs=zero[:], start=True, stop=True)
+
+        keep_warm(WARM[0])
         wro = const.tile([P, 4096], BF16, name="wro")
         wx = const.tile([P, 4096], BF16, name="wx")
 
@@ -158,6 +169,7 @@ def tile_snnlayer_pa_t_kernel(
                 for m2 in range(2):
                     for u in range(2):
                         nc.tensor.transpose(ptv[:, m2, u, :], w_words(c, 2 * jj + m2, u), ident[:])
+                keep_warm(WARM[1 + ci])
                 dst = gw_f[:, 2 * jj : 2 * jj + 2, :, :]
                 srcv = ptv.rearrange("q m u n -> q m n u")
                 if jj == 0 or ci > 1:
@@ -247,6 +259,8 @@ def tile_snnlayer_pa_t_kernel(
                     for t in range(NT):
                         for u in range(2):
                             nc.tensor.transpose(ptv[:, t, u, :], src_f[:, t, woff + P * u : woff + P * u + P], ident[:])
+                    if n < 4:
+                        keep_warm(WARM[5 + n])
                     s_copies.append(
                         (
                             grt[:].bitcast(F32)[:, c2 * 512 : (c2 + 1) * 512].rearrange("q (t i u) -> q t i u", t=NT, i=P, u=2),

@@ -25,9 +25,13 @@ OFF_MX = 2
 OFF_BK = 5
 MN_LEAD = 4
 GR_BUFS = 4
-WARM = (6, 2, 2, 1, 1, 1, 1, 1, 0)
+WARM = (3, 2, 2, 1, 1, 1, 1, 1, 0)
 A_UNIT = 2
-WX_UNIT = 1
+W_UNITS = ((1, ((2, 0), (3, 0), (0, 1), (1, 1))), (2, ((2, 1), (3, 1))))
+W_VECTOR = ()
+WARM_1 = 1
+B_FIRST = True
+LOAD_ORDER = ("ss", "xs", "bs", "ms")
 N_UNITS = 2 * (G - 1) + OFF_BK + 3
 
 
@@ -64,16 +68,18 @@ def tile_snnlayer_pa_t_kernel(
             v = loaded[(g // 2, nm)][:].rearrange("p t k -> p (t k)").bitcast(F32).rearrange("p (t w) -> p t w", t=2 * NT)
             return v[:, (g % 2) * NT : (g % 2 + 1) * NT, :]
 
+        zero = const.tile([P, 512], BF16, name="zero")
+        nc.vector.memset(zero[:], 0.0)
         craw = const.tile([P, 256], BF16, name="craw")
         nc.vector.memset(craw[:], 0.0)
         ident = const.tile([P, P], F32, name="ident")
         make_identity(nc, ident[:])
-        zero = const.tile([P, 512], BF16, name="zero")
-        nc.vector.memset(zero[:], 0.0)
+        scr = const.tile([P, 1], F32, name="scr")
+        nc.scalar.activation(out=scr[:], in_=zero[:, 0:1], func=ACT.Sigmoid)
 
         def keep_warm(count):
             if count:
-                warm = bank("warm", "bk", 2)
+                warm = bank("warm", "mx", 2)
                 for i in range(count):
                     nc.tensor.matmul(warm[:], lhsT=zero[:, 0:P], rhs=zero[:], start=True, stop=True)
 
@@ -81,23 +87,32 @@ def tile_snnlayer_pa_t_kernel(
         wro = const.tile([P, 4096], BF16, name="wro")
         wx = const.tile([P, 4096], BF16, name="wx")
 
-        def w_load(dst, src):
+        def w_load(dst, src, u):
             dst_v = dst.rearrange("p (u e k) -> p u e k", u=2, e=2)
             src_v = src.rearrange("(u p e) k -> p u e k", u=2, p=P, e=2)
-            for u in range(2):
-                nc.sync.dma_start(out=dst_v[:, u], in_=src_v[:, u])
+            nc.sync.dma_start(out=dst_v[:, u], in_=src_v[:, u])
 
-        w_load(wro[:, 0:2048], W_rec4in)
+        w_load(wro[:, 0:2048], W_rec4in, 0)
         for v, vec in enumerate((b_x2in, b_rec4in, b_out2in, tau_adp_in, tau_m_in)):
             nc.sync.dma_start(out=craw[2 * v : 2 * v + 2, :], in_=vec.rearrange("(u w) -> u w", u=2))
-        w_load(wro[:, 2048:4096], W_out2in)
+        w_load(wro[:, 2048:4096], W_out2in, 0)
         load(0, "ss", 0)
-        w_load(wx[:], W_x2in)
+        w_load(wx[:], W_x2in, 0)
+        load(0, "xs", 0)
+        w_load(wro[:, 0:2048], W_rec4in, 1)
+        w_load(wro[:, 2048:4096], W_out2in, 1)
+        if B_FIRST:
+            load(0, "bs", 0)
+        w_load(wx[:], W_x2in, 1)
+        if not B_FIRST:
+            load(0, "bs", 0)
+        for nm in ("ss", "xs", "bs"):
+            load(0, nm, 1)
         for part in range(2):
-            for nm in ("xs", "bs", "ms") if part == 0 else ("ss", "xs", "bs", "ms"):
-                load(0, nm, part)
-        for nm in ("ss", "bs", "xs", "ms"):
-            load(1, nm)
+            load(0, "ms", part)
+            for nm in ("ss", "xs", "bs"):
+                load(1, nm, part)
+        load(1, "ms")
 
         cst = const.tile([P, 20], F32, name="cst")
         bsum = const.tile([P, 4], F32, name="bsum")
@@ -137,8 +152,8 @@ def tile_snnlayer_pa_t_kernel(
                 in_=aps[:].rearrange("i (u e q) -> i u q e", u=2, e=2, q=P),
             )
 
-        wcodes = const.tile([P, 16 * P], U32, name="wcodes", align_bytes=64)
-        wscales = const.tile([P, 16 * P], U8, name="wscales", align_bytes=64)
+        wcodes = const.tile([P, 16 * P], U32, name="wcodes", align_bytes=256)
+        wscales = const.tile([P, 16 * P], U8, name="wscales", align_bytes=256)
         wx_f = wx[:].bitcast(F32)
         wro_f = wro[:].bitcast(F32)
 
@@ -151,37 +166,32 @@ def tile_snnlayer_pa_t_kernel(
 
         gws = {}
 
-        def w_quantise(ci):
-            nc.vector.quantize_mx(
-                out=wcodes[:, ci * 512 : (ci + 1) * 512].bitcast(FP8X4),
-                scales=wscales[:, ci * 512 : (ci + 1) * 512],
-                in_=gws[ci][:],
-            )
-
-        def weights(ci):
+        def weights(ci, v):
             c = PASS_ORDER[ci]
-            gw = qp.tile([P, 2048], BF16, name="gw", tag="gr%d" % (ci // 2), align_bytes=64)
-            gws[ci] = gw
-            gw_f = gw[:].bitcast(F32).rearrange("q (m n u) -> q m n u", m=4, n=P, u=2)
-            for jj in range(2):
-                pt = bank("wt", "tx", 3)
-                ptv = pt[:].rearrange("q (m u n) -> q m u n", m=2, u=2, n=P)
-                for m2 in range(2):
-                    for u in range(2):
-                        nc.tensor.transpose(ptv[:, m2, u, :], w_words(c, 2 * jj + m2, u), ident[:])
-                keep_warm(WARM[1 + ci])
-                dst = gw_f[:, 2 * jj : 2 * jj + 2, :, :]
-                srcv = ptv.rearrange("q m u n -> q m n u")
-                if jj == 0 or ci > 1:
-                    nc.scalar.copy(out=dst, in_=srcv)
-                else:
-                    nc.vector.tensor_copy(out=dst, in_=srcv)
+            gw = qp.tile([P, 1024], BF16, name="gw", tag="gw", bufs=4, align_bytes=256)
+            gws[(ci, v)] = gw
+            pt = bank("wt", "tx", 3)
+            ptv = pt[:].rearrange("q (m u n) -> q m u n", m=2, u=2, n=P)
+            for m2 in range(2):
+                for u in range(2):
+                    nc.tensor.transpose(ptv[:, m2, u, :], w_words(c, 2 * v + m2, u), ident[:])
+            keep_warm(WARM[1 + ci] if v == 0 else WARM_1)
+            dst = gw[:].bitcast(F32).rearrange("q (m n u) -> q m n u", m=2, n=P, u=2)
+            srcv = ptv.rearrange("q m u n -> q m n u")
+            if (ci, v) in W_VECTOR:
+                nc.vector.tensor_copy(out=dst, in_=srcv)
+            else:
+                nc.scalar.copy(out=dst, in_=srcv)
 
-        weights(0)
+        def w_quantise(ci, v):
+            cols = slice(ci * 512 + v * 256, ci * 512 + (v + 1) * 256)
+            nc.vector.quantize_mx(out=wcodes[:, cols].bitcast(FP8X4), scales=wscales[:, cols], in_=gws[(ci, v)][:])
+
+        weights(0, 0)
         make_constants()
-        weights(1)
-        w_quantise(0)
-        w_quantise(1)
+        weights(1, 0)
+        w_quantise(0, 0)
+        w_quantise(1, 0)
 
         gr, ac, accs, tmb, mts, mns, bks, obs = {}, {}, {}, {}, {}, {}, {}, {}
 
@@ -190,20 +200,21 @@ def tile_snnlayer_pa_t_kernel(
                 d = n - age
                 return (d // 2, d % 2) if 0 <= d < 2 * G else None
 
-            load(n // 4 + 2, ("ss", "bs", "xs", "ms")[n % 4])
+            load(n // 4 + 2, LOAD_ORDER[n % 4])
 
-            if n == WX_UNIT:
-                weights(2)
-                weights(3)
-                w_quantise(2)
-                w_quantise(3)
+            for wn, ws in W_UNITS:
+                if n == wn:
+                    for ci, v in ws:
+                        weights(ci, v)
+                    for ci, v in ws:
+                        w_quantise(ci, v)
             if n == A_UNIT:
                 make_a_nat()
 
             if at(1):
                 g, h = at(1)
-                a_c = qp.tile([P, 2 * NS], U32, name="ac%d" % h, tag="ac%d" % h, align_bytes=64)
-                a_s = qp.tile([P, 2 * NS], U8, name="as%d" % h, tag="as%d" % h, align_bytes=64)
+                a_c = qp.tile([P, 2 * NS], U32, name="ac%d" % h, tag="ac%d" % h, align_bytes=256)
+                a_s = qp.tile([P, 2 * NS], U8, name="as%d" % h, tag="as%d" % h, align_bytes=256)
                 nc.vector.quantize_mx(out=a_c[:].bitcast(FP8X4), scales=a_s[:], in_=gr[(g, h)][:])
                 ac[(g, h)] = (a_c, a_s)
             i = n - OFF_BK - 1 + MN_LEAD
@@ -248,7 +259,7 @@ def tile_snnlayer_pa_t_kernel(
             s_copies = []
             if at(0):
                 g, h = at(0)
-                grt = qp.tile([P, 2 * 4 * NS], BF16, name="gr%d" % h, tag="gr%d" % h, align_bytes=64)
+                grt = qp.tile([P, 2 * 4 * NS], BF16, name="gr%d" % h, tag="gr%d" % h, align_bytes=256)
                 gr[(g, h)] = grt
                 for c2 in range(2):
                     c = PASS_ORDER[2 * h + c2]

@@ -25,11 +25,9 @@ OFF_MX = 2
 OFF_BK = 5
 MN_LEAD = 4
 GR_BUFS = 4
-WARM = (3, 2, 2, 1, 1, 1, 1, 1, 0)
 A_UNIT = 2
 W_UNITS = ((1, ((2, 0), (3, 0), (0, 1), (1, 1))), (2, ((2, 1), (3, 1))))
 W_VECTOR = ()
-WARM_1 = 1
 B_FIRST = True
 LOAD_ORDER = ("ss", "xs", "bs", "ms")
 N_UNITS = 2 * (G - 1) + OFF_BK + 3
@@ -77,13 +75,6 @@ def tile_snnlayer_pa_t_kernel(
         scr = const.tile([P, 1], F32, name="scr")
         nc.scalar.activation(out=scr[:], in_=zero[:, 0:1], func=ACT.Sigmoid)
 
-        def keep_warm(count):
-            if count:
-                warm = bank("warm", "mx", 2)
-                for i in range(count):
-                    nc.tensor.matmul(warm[:], lhsT=zero[:, 0:P], rhs=zero[:], start=True, stop=True)
-
-        keep_warm(WARM[0])
         wro = const.tile([P, 4096], BF16, name="wro")
         wx = const.tile([P, 4096], BF16, name="wx")
 
@@ -175,7 +166,6 @@ def tile_snnlayer_pa_t_kernel(
             for m2 in range(2):
                 for u in range(2):
                     nc.tensor.transpose(ptv[:, m2, u, :], w_words(c, 2 * v + m2, u), ident[:])
-            keep_warm(WARM[1 + ci] if v == 0 else WARM_1)
             dst = gw[:].bitcast(F32).rearrange("q (m n u) -> q m n u", m=2, n=P, u=2)
             srcv = ptv.rearrange("q m u n -> q m n u")
             if (ci, v) in W_VECTOR:
@@ -270,8 +260,6 @@ def tile_snnlayer_pa_t_kernel(
                     for t in range(NT):
                         for u in range(2):
                             nc.tensor.transpose(ptv[:, t, u, :], src_f[:, t, woff + P * u : woff + P * u + P], ident[:])
-                    if n < 4:
-                        keep_warm(WARM[5 + n])
                     s_copies.append(
                         (
                             grt[:].bitcast(F32)[:, c2 * 512 : (c2 + 1) * 512].rearrange("q (t i u) -> q t i u", t=NT, i=P, u=2),

from contextlib import ExitStack

import concourse.mybir as mybir
from concourse.masks import make_identity

F32 = mybir.dt.float32
BF16 = mybir.dt.bfloat16
U32 = mybir.dt.uint32
U8 = mybir.dt.uint8
FP8X4 = mybir.dt.float8_e4m3fn_x4
ALU = mybir.AluOpType
ACT = mybir.ActivationFunctionType

P = 128
B, IN_DIM, R_IN = 4096, 1024, 512
FLOPS = 2 * B * (IN_DIM + 2 * R_IN) * R_IN

NT = 2
NS = NT * P
G = B // NS
PASS_ORDER = (3, 2, 0, 1)
OFF_Z = 1
OFF_Z2 = 2
OFF_MX = 2
OFF_BK = 5
MN_LEAD = 4
GR_BUFS = 4
A_UNIT = 2
W_UNITS = ((1, ((2, 0), (3, 0), (0, 1), (1, 1))), (2, ((2, 1), (3, 1))))
W_VECTOR = ()
B_FIRST = True
LOAD_ORDER = ("ss", "xs", "bs", "ms")
N_UNITS = 2 * (G - 1) + OFF_BK + 3


def tile_snnlayer_pa_t_kernel(
    tc, x_t, spk_t, mem_t_in, b_t_in, W_x2in, b_x2in, W_rec4in, b_rec4in, W_out2in, b_out2in, tau_adp_in, tau_m_in, out
):
    nc = tc.nc
    with ExitStack() as ctx:
        ctx.enter_context(tc.manual_schedule())
        const = ctx.enter_context(tc.tile_pool(name="const", bufs=1))
        ld = ctx.enter_context(tc.tile_pool(name="ld", bufs=3))
        qp = ctx.enter_context(tc.tile_pool(name="qp", bufs=GR_BUFS))
        ep = ctx.enter_context(tc.tile_pool(name="ep", bufs=2))
        ps = ctx.enter_context(tc.psum_pool(name="ps", bufs=1))

        def bank(name, tag, bufs):
            return ps.tile([P, 512], F32, name=name, tag=tag, bufs=bufs)

        srcs = {"ss": (spk_t, 1024), "xs": (x_t, 1024), "bs": (b_t_in, 512), "ms": (mem_t_in, 512)}
        loaded = {}

        def load(pair, nm, part=None):
            if 2 * pair >= G:
                return
            src, width = srcs[nm]
            if part in (None, 0):
                loaded[(pair, nm)] = ld.tile([P, 2 * NT, width], BF16, name=nm, tag=nm)
            dst = loaded[(pair, nm)]
            src_v = src[2 * pair * NS : 2 * (pair + 1) * NS, :].rearrange("(p t) k -> p t k", t=2 * NT)
            lo, hi = (0, 2 * NT) if part is None else (part * NT, (part + 1) * NT)
            nc.sync.dma_start(out=dst[:, lo:hi, :], in_=src_v[:, lo:hi, :])

        def words(g, nm):
            v = loaded[(g // 2, nm)][:].rearrange("p t k -> p (t k)").bitcast(F32).rearrange("p (t w) -> p t w", t=2 * NT)
            return v[:, (g % 2) * NT : (g % 2 + 1) * NT, :]

        zero = const.tile([P, 512], BF16, name="zero")
        nc.vector.memset(zero[:], 0.0)
        craw = const.tile([P, 256], BF16, name="craw")
        nc.vector.memset(craw[:], 0.0)
        ident = const.tile([P, P], F32, name="ident")
        make_identity(nc, ident[:])
        scr = const.tile([P, 1], F32, name="scr")
        nc.scalar.activation(out=scr[:], in_=zero[:, 0:1], func=ACT.Sigmoid)

        wro = const.tile([P, 4096], BF16, name="wro")
        wx = const.tile([P, 4096], BF16, name="wx")

        def w_load(dst, src, u):
            dst_v = dst.rearrange("p (u e k) -> p u e k", u=2, e=2)
            src_v = src.rearrange("(u p e) k -> p u e k", u=2, p=P, e=2)
            nc.sync.dma_start(out=dst_v[:, u], in_=src_v[:, u])

        w_load(wro[:, 0:2048], W_rec4in, 0)
        for v, vec in enumerate((b_x2in, b_rec4in, b_out2in, tau_adp_in, tau_m_in)):
            nc.sync.dma_start(out=craw[2 * v : 2 * v + 2, :], in_=vec.rearrange("(u w) -> u w", u=2))
        w_load(wro[:, 2048:4096], W_out2in, 0)
        load(0, "ss", 0)
        w_load(wx[:], W_x2in, 0)
        load(0, "xs", 0)
        w_load(wro[:, 0:2048], W_rec4in, 1)
        w_load(wro[:, 2048:4096], W_out2in, 1)
        if B_FIRST:
            load(0, "bs", 0)
        w_load(wx[:], W_x2in, 1)
        if not B_FIRST:
            load(0, "bs", 0)
        for nm in ("ss", "xs", "bs"):
            load(0, nm, 1)
        for part in range(2):
            load(0, "ms", part)
            for nm in ("ss", "xs", "bs"):
                load(1, nm, part)
        load(1, "ms")

        cst = const.tile([P, 20], F32, name="cst")
        bsum = const.tile([P, 4], F32, name="bsum")
        sg = const.tile([P, 8], F32, name="sg")
        ng = const.tile([P, 8], F32, name="ng")
        md = const.tile([P, 4], F32, name="md")
        mc = const.tile([P, 4], F32, name="mc")
        dd = const.tile([P, 4], F32, name="dd")
        rr = const.tile([P, 4], F32, name="rr")
        c3 = const.tile([P, 4], F32, name="c3")
        k0 = const.tile([P, 4], F32, name="k0")
        aa = sg[:, 4:8]
        a_nat = const.tile([P, R_IN], F32, name="a_nat")

        def make_constants():
            cps = bank("cps", "tx", 3)
            nc.tensor.transpose(cps[:, 0:P], craw[:].bitcast(F32), ident[:])
            nc.vector.tensor_copy(out=cst[:], in_=cps[:].bitcast(BF16)[:, 0:20])
            nc.vector.tensor_add(out=bsum[:], in0=cst[:, 0:4], in1=cst[:, 4:8])
            nc.vector.tensor_add(out=bsum[:], in0=bsum[:], in1=cst[:, 8:12])
            nc.scalar.activation(out=sg[:], in_=cst[:, 12:20], func=ACT.Sigmoid)
            nc.scalar.activation(out=ng[:], in_=cst[:, 12:20], func=ACT.Sigmoid, scale=-1.0)
            nc.vector.tensor_scalar(out=mc[:], in0=ng[:, 0:4], scalar1=1.8, scalar2=0.1, op0=ALU.mult, op1=ALU.add)
            nc.vector.tensor_scalar(out=dd[:], in0=sg[:, 0:4], scalar1=1.8, scalar2=1e-30, op0=ALU.mult, op1=ALU.max)
            nc.scalar.mul(out=md[:], in_=dd[:], mul=-1.0)
            nc.vector.reciprocal(out=rr[:], in_=dd[:])
            nc.vector.tensor_mul(out=rr[:], in0=mc[:], in1=rr[:])
            nc.scalar.mul(out=c3[:], in_=ng[:, 4:8], mul=3.0)
            nc.vector.tensor_mul(out=k0[:], in0=c3[:], in1=bsum[:])

        def make_a_nat():
            aps = bank("aps", "bk", 2)
            for j in range(4):
                nc.tensor.transpose(aps[:, j * P : (j + 1) * P], aa[:, j : j + 1].to_broadcast([P, P]), ident[:])
            nc.vector.tensor_copy(
                out=a_nat[:].rearrange("i (u q e) -> i u q e", u=2, q=P, e=2),
                in_=aps[:].rearrange("i (u e q) -> i u q e", u=2, e=2, q=P),
            )

        wcodes = const.tile([P, 16 * P], U32, name="wcodes", align_bytes=256)
        wscales = const.tile([P, 16 * P], U8, name="wscales", align_bytes=256)
        wx_f = wx[:].bitcast(F32)
        wro_f = wro[:].bitcast(F32)

        def w_words(c, j, u):
            if c < 2:
                lo = j * 512 + 256 * c + P * u
                return wx_f[:, lo : lo + P]
            lo = (0 if c == 3 else 1024) + j * 256 + P * u
            return wro_f[:, lo : lo + P]

        gws = {}

        def weights(ci, v):
            c = PASS_ORDER[ci]
            gw = qp.tile([P, 1024], BF16, name="gw", tag="gw", bufs=4, align_bytes=256)
            gws[(ci, v)] = gw
            pt = bank("wt", "tx", 3)
            ptv = pt[:].rearrange("q (m u n) -> q m u n", m=2, u=2, n=P)
            for m2 in range(2):
                for u in range(2):
                    nc.tensor.transpose(ptv[:, m2, u, :], w_words(c, 2 * v + m2, u), ident[:])
            dst = gw[:].bitcast(F32).rearrange("q (m n u) -> q m n u", m=2, n=P, u=2)
            srcv = ptv.rearrange("q m u n -> q m n u")
            if (ci, v) in W_VECTOR:
                nc.vector.tensor_copy(out=dst, in_=srcv)
            else:
                nc.scalar.copy(out=dst, in_=srcv)

        def w_quantise(ci, v):
            cols = slice(ci * 512 + v * 256, ci * 512 + (v + 1) * 256)
            nc.vector.quantize_mx(out=wcodes[:, cols].bitcast(FP8X4), scales=wscales[:, cols], in_=gws[(ci, v)][:])

        weights(0, 0)
        make_constants()
        weights(1, 0)
        w_quantise(0, 0)
        w_quantise(1, 0)

        gr, ac, accs, tmb, mts, mns, bks, obs = {}, {}, {}, {}, {}, {}, {}, {}

        for n in range(N_UNITS):
            def at(age):
                d = n - age
                return (d // 2, d % 2) if 0 <= d < 2 * G else None

            load(n // 4 + 2, LOAD_ORDER[n % 4])

            for wn, ws in W_UNITS:
                if n == wn:
                    for ci, v in ws:
                        weights(ci, v)
                    for ci, v in ws:
                        w_quantise(ci, v)
            if n == A_UNIT:
                make_a_nat()

            if at(1):
                g, h = at(1)
                a_c = qp.tile([P, 2 * NS], U32, name="ac%d" % h, tag="ac%d" % h, align_bytes=256)
                a_s = qp.tile([P, 2 * NS], U8, name="as%d" % h, tag="as%d" % h, align_bytes=256)
                nc.vector.quantize_mx(out=a_c[:].bitcast(FP8X4), scales=a_s[:], in_=gr[(g, h)][:])
                ac[(g, h)] = (a_c, a_s)
            i = n - OFF_BK - 1 + MN_LEAD
            if 0 <= i < 2 * G:
                if at(1):
                    mn = gr[at(1)][:, 4 * NS : 8 * NS].bitcast(F32)
                else:
                    mn = ep.tile([P, R_IN], F32, name="mn", tag="mn", bufs=2)
                    mn = mn[:]
                mns[i] = mn
                nc.gpsimd.tensor_tensor(out=mn, in0=loaded[(i // 4, "ms")][:, i % 4, :], in1=a_nat[:], op=ALU.mult)

            if at(OFF_BK + 1):
                g, t = at(OFF_BK + 1)
                if t == 0:
                    obs[g] = ep.tile([P, NT, R_IN], F32, name="ob", tag="ob", bufs=4)
                ob = obs[g]
                nc.vector.tensor_tensor(
                    out=ob[:, t, :].rearrange("i (u q e) -> i u q e", u=2, q=P, e=2),
                    in0=bks[(g, t)][:].rearrange("i (u e q) -> i u q e", u=2, e=2, q=P),
                    in1=mns[2 * g + t].rearrange("i (u q e) -> i u q e", u=2, q=P, e=2),
                    op=ALU.add,
                )
                lo, hi = (t, t + 1) if g == G - 1 else (0, NT)
                if t == NT - 1 or g == G - 1:
                    out_v = out[2 * (g // 2) * NS : 2 * (g // 2 + 1) * NS, :].rearrange("(p t) n -> p t n", t=2 * NT)
                    nc.sync.dma_start(out=out_v[:, (g % 2) * NT + lo : (g % 2) * NT + hi, :], in_=ob[:, lo:hi, :])
            if at(OFF_MX + 1):
                g, u = at(OFF_MX + 1)
                mt = mts[(g, u)]
                for e in range(2):
                    j = 2 * u + e
                    nc.vector.scalar_tensor_tensor(
                        out=mt[:, e, :],
                        in0=accs[(g, u)][:, e * NS : (e + 1) * NS],
                        scalar=c3[:, j : j + 1],
                        in1=mt[:, e, :],
                        op0=ALU.mult,
                        op1=ALU.add,
                    )

            s_copies = []
            if at(0):
                g, h = at(0)
                grt = qp.tile([P, 2 * 4 * NS], BF16, name="gr%d" % h, tag="gr%d" % h, align_bytes=256)
                gr[(g, h)] = grt
                for c2 in range(2):
                    c = PASS_ORDER[2 * h + c2]
                    src_f = words(g, "xs" if c < 2 else "ss")
                    woff = 256 * (c % 2)
                    pt = bank("xt", "tx", 3)
                    ptv = pt[:].rearrange("q (t u i) -> q t u i", t=NT, u=2, i=P)
                    for t in range(NT):
                        for u in range(2):
                            nc.tensor.transpose(ptv[:, t, u, :], src_f[:, t, woff + P * u : woff + P * u + P], ident[:])
                    s_copies.append(
                        (
                            grt[:].bitcast(F32)[:, c2 * 512 : (c2 + 1) * 512].rearrange("q (t i u) -> q t i u", t=NT, i=P, u=2),
                            ptv.rearrange("q t u i -> q t i u"),
                        )
                    )
            if at(OFF_Z):
                g, u = at(OFF_Z)
                pb = bank("pb", "tm", 1)
                for t in range(NT):
                    nc.tensor.transpose(pb[:, t * P : (t + 1) * P], words(g, "bs")[:, t, P * u : P * u + P], ident[:])
                tmb[(g, u)] = pb
            if at(OFF_BK):
                g, t = at(OFF_BK)
                bk = bank("bk", "bk", 2)
                bkv = bk[:].rearrange("i (j q) -> i j q", j=4)
                for j in range(4):
                    nc.tensor.transpose(bkv[:, j, :], mts[(g, j // 2)][:, j % 2, t * P : (t + 1) * P], ident[:])
                bks[(g, t)] = bk

            if at(OFF_MX):
                g, u = at(OFF_MX)
                acc = bank("acc", "mx", 2)
                accs[(g, u)] = acc
                for e in range(2):
                    j = 2 * u + e
                    for ci in range(4):
                        a_c, a_s = ac[(g, ci // 2)]
                        o = (ci % 2) * NS
                        w0 = (ci * 4 + j) * P
                        nc.tensor.matmul_mx(
                            out=acc[:, e * NS : (e + 1) * NS],
                            lhsT=wcodes[:, w0 : w0 + P].bitcast(FP8X4),
                            lhsT_scale=wscales[:, w0 : w0 + P],
                            rhs=a_c[:, o : o + NS].bitcast(FP8X4),
                            rhs_scale=a_s[:, o : o + NS],
                            start=(ci == 0),
                            stop=(ci == 3),
                        )

            for dst, srcv in s_copies:
                nc.scalar.copy(out=dst, in_=srcv)
            if at(OFF_Z2):
                g, u = at(OFF_Z2)
                mt = mts[(g, u)]
                for e in range(2):
                    j = 2 * u + e
                    nc.scalar.activation(out=mt[:, e, :], in_=mt[:, e, :], func=ACT.Identity, bias=k0[:, j : j + 1], scale=md[:, j : j + 1])

            if at(OFF_Z):
                g, u = at(OFF_Z)
                mt = ep.tile([P, 2, NS], F32, name="mt", tag="mt", bufs=8)
                mts[(g, u)] = mt
                btv = tmb[(g, u)][:, 0:NS].bitcast(BF16).rearrange("q (s e) -> q s e", e=2)
                spk4 = gr[(g, 0)][:, 0 : 4 * NS].rearrange("q (s t) -> q s t", t=4)
                for e in range(2):
                    j = 2 * u + e
                    nc.vector.scalar_tensor_tensor(
                        out=mt[:, e, :], in0=btv[:, :, e], scalar=rr[:, j : j + 1], in1=spk4[:, :, j], op0=ALU.add, op1=ALU.mult
                    )
